import numpy as np
import ml_dtypes


def mxq(x, axis, fmt="e4m3"):
    dtype, down = {"e4m3": (ml_dtypes.float8_e4m3fn, 7), "e5m2": (ml_dtypes.float8_e5m2, 14)}[fmt]
    v = np.moveaxis(np.asarray(x, np.float32).astype(ml_dtypes.bfloat16).astype(np.float64), axis, -1)
    blocks = v.reshape(v.shape[:-1] + (-1, 32))
    amax = np.abs(blocks).max(-1, keepdims=True)
    byte = np.maximum(np.where(amax > 0, np.frexp(amax)[1] - 1 + 127, 0) - down, 1)
    scale = np.exp2(byte - 127.0)
    codes = (blocks / scale).astype(np.float32).astype(dtype).astype(np.float64)
    return np.moveaxis((codes * scale).reshape(v.shape), -1, axis)


WIDE = False


def mx_kscale(k):
    if not WIDE:
        return np.ones(k)
    levels = np.array([10, -10, 5, -5, 0])
    a = np.random.permutation(np.resize(levels, k // 512 * 4)).reshape(k // 512, 4)
    idx = np.arange(k)
    return np.exp2(a[idx // 512, idx % 128 // 32])


BF16 = ml_dtypes.bfloat16


def bf(x):
    return np.asarray(x, np.float32).astype(BF16)


def f64(x):
    return np.asarray(x).astype(np.float64)


B, S, H, KV, D, W, META = 4, 1024, 4, 1, 128, 256, 4
BLK = 32


def swa_sink_mask():
    i = np.arange(S)[:, None]
    j = np.arange(S)[None, :]
    return (i >= j) & (((i - j) <= W) | (j < META))


def setup_inputs():
    s = np.array(mx_kscale(S), dtype=np.float64)
    s[:BLK] = s.max()
    q = np.random.standard_normal((B, S, H, D))
    k = np.random.standard_normal((B, S, KV, D))
    v = np.random.standard_normal((B, S, KV, D)) * 2.0
    q[..., 0] = np.log(2.0) * np.sqrt(D)
    k[..., 0] += np.log2(s)[None, :, None]
    v *= (s.max() / s)[None, :, None, None]
    return {"query_states": bf(q.reshape(B, S, H * D)),
            "key_states": bf(k.reshape(B, S, KV * D)),
            "value_states": bf(v.reshape(B, S, KV * D))}


def reference(query_states, key_states, value_states):
    q = f64(query_states).reshape(B, S, H, D).transpose(0, 2, 1, 3)
    k = f64(key_states).reshape(B, S, KV, D).transpose(0, 2, 1, 3)
    v = f64(value_states).reshape(B, S, KV, D).transpose(0, 2, 1, 3)
    k = np.repeat(k, H // KV, axis=1)
    v = np.repeat(v, H // KV, axis=1)
    scores = (q @ k.transpose(0, 1, 3, 2)) * (1.0 / np.sqrt(D))
    scores = np.where(swa_sink_mask()[None, None], scores, -np.inf)
    e = np.exp(scores - scores.max(-1, keepdims=True))
    out = (mxq(e, 3, "e4m3") @ mxq(v, 2, "e4m3")) / e.sum(-1, keepdims=True)
    return out.transpose(0, 2, 1, 3).reshape(B, S, H * D)

@@ -1,0 +1,355 @@
+from contextlib import ExitStack
+import math
+
+import concourse.mybir as mybir
+from concourse.masks import make_identity
+
+BF16 = mybir.dt.bfloat16
+F32 = mybir.dt.float32
+I32 = mybir.dt.int32
+U32 = mybir.dt.uint32
+U8 = mybir.dt.uint8
+FP8X4 = mybir.dt.float8_e4m3fn_x4
+ALU = mybir.AluOpType
+ACTF = mybir.ActivationFunctionType
+AX = mybir.AxisListType
+
+B, S, H, D, WIN, META = 4, 1024, 4, 128, 256, 4
+P = 128
+BLK = 32
+POS = P // H
+NT = S // POS
+UNITS = B * NT
+PAIRS = UNITS // 2
+RUN = 10
+SCALE = 1.0 / math.sqrt(D)
+NEG = -1.0e30
+ALLOWED = sum(min(i, WIN) + 1 + min(max(i - WIN, 0), META) for i in range(S))
+FLOPS = 4 * D * ALLOWED * B * H
+
+BASES = (2, 9, 16, 17)
+OPER = [list(range(16))] + [
+    list(range(c, c + 8)) + [0] + list(range(c + 8, c + 15)) for c in BASES
+]
+K_FIRST, K_LAST, K_SINK, K_FIRST8 = 0, 1, 2, 3
+RG_V_EVERY = 1000
+
+
+def plan(t):
+    if t <= 9:
+        o, a, n = 0, 0, min(t, 9) + 1
+    elif t <= 16:
+        o, a, n = 1, t - 10, RUN
+    elif t <= 23:
+        o, a, n = 2, t - 17, RUN
+    elif t <= 30:
+        o, a, n = 3, t - 24, RUN
+    else:
+        o, a, n = 4, 6, RUN
+    slots = OPER[o][a : a + n]
+    segs = []
+    bmasks = []
+    for idx, kb in enumerate(slots):
+        if segs and kb == segs[-1][1] + segs[-1][2]:
+            segs[-1][2] += 1
+        else:
+            segs.append([idx, kb, 1])
+        if kb == t:
+            bmasks.append((idx, K_LAST))
+        elif kb == t - 8:
+            bmasks.append((idx, K_FIRST8 if kb == 0 else K_FIRST))
+        elif kb == 0 and t > 8:
+            bmasks.append((idx, K_SINK))
+        else:
+            assert t - 8 < kb < t
+    return o, a, n, segs, bmasks
+
+
+def tile_swa_sinkmeta_t_kernel(tc, query_states, key_states, value_states, out):
+    nc = tc.nc
+    with ExitStack() as ctx:
+        ctx.enter_context(tc.manual_schedule())
+        const = ctx.enter_context(tc.tile_pool(name="const", bufs=1))
+        qtp = ctx.enter_context(tc.tile_pool(name="qtp", bufs=5))
+        grpp = ctx.enter_context(tc.tile_pool(name="grpp", bufs=3))
+        codp = ctx.enter_context(tc.tile_pool(name="codp", bufs=3))
+        osbp = ctx.enter_context(tc.tile_pool(name="osbp", bufs=8))
+        small = ctx.enter_context(tc.tile_pool(name="small", bufs=8))
+        ps_s = ctx.enter_context(tc.psum_pool(name="ps_s", bufs=4))
+        ps_t = ctx.enter_context(tc.psum_pool(name="ps_t", bufs=2))
+        ps_a = ctx.enter_context(tc.psum_pool(name="ps_a", bufs=1))
+        ps_o = ctx.enter_context(tc.psum_pool(name="ps_o", bufs=1))
+
+        q_view = query_states.rearrange("b s c -> (b s c)").rearrange(
+            "(n r d) -> r n d", r=P, d=D
+        )
+        o_view = out.rearrange("b s c -> (b s c)").rearrange("(n r d) -> r n d", r=P, d=D)
+        k_view = key_states.rearrange("b (a p) d -> p (b a) d", p=P)
+
+        def v_rows(k0, nkeys):
+            return value_states[:, k0 : k0 + nkeys, :].rearrange("b (p t) d -> p b (t d)", t=4)
+
+        k_sb = [const.tile([P, 8, D], BF16, name="k_sb%d" % b) for b in range(B)]
+        q_sb = [const.tile([P, 8, D], BF16, name="q_sb%d" % c) for c in range(UNITS // 8)]
+        v_raw = [const.tile([P, B, 4 * D], BF16, name="v_raw%d" % o) for o in range(5)]
+
+        def load_k(b):
+            nc.sync.dma_start(out=k_sb[b][:], in_=k_view[:, 8 * b : 8 * b + 8, :])
+
+        def load_q(c):
+            nc.sync.dma_start(out=q_sb[c][:], in_=q_view[:, 8 * c : 8 * c + 8, :])
+
+        def load_v(o):
+            if o == 0:
+                nc.sync.dma_start(out=v_raw[0][:], in_=v_rows(0, 512))
+            else:
+                c = BASES[o - 1]
+                nc.sync.dma_start(out=v_raw[o][0:64], in_=v_rows(BLK * c, 256))
+                nc.sync.dma_start(out=v_raw[o][64:72], in_=v_rows(0, BLK))
+                nc.sync.dma_start(out=v_raw[o][72:128], in_=v_rows(BLK * (c + 8), 224))
+
+        load_k(0)
+        load_q(0)
+        load_v(0)
+        load_q(1)
+        load_v(1)
+        load_q(2)
+        load_v(2)
+        load_q(3)
+        load_v(3)
+        load_v(4)
+        for b in range(1, B):
+            load_k(b)
+            for c in range(4 * b, 4 * b + 4):
+                load_q(c)
+
+        ident = const.tile([P, P], BF16, name="ident")
+        make_identity(nc, ident[:])
+        mask_f = const.tile([P, 2, BLK], F32, name="mask_f")
+        nc.gpsimd.memset(mask_f[:], 0.0)
+        nc.gpsimd.affine_select(
+            out=mask_f[:, 0, :], in_=mask_f[:, 0, :], compare_op=ALU.is_ge, fill=NEG,
+            base=3, pattern=[[4, BLK]], channel_multiplier=-1,
+        )
+        nc.gpsimd.affine_select(
+            out=mask_f[:, 1, :], in_=mask_f[:, 1, :], compare_op=ALU.is_ge, fill=NEG,
+            base=0, pattern=[[-4, BLK]], channel_multiplier=1,
+        )
+
+        warm = const.tile([P, 1], F32, name="warm")
+        nc.vector.memset(warm[:], 0.0)
+        nc.scalar.activation(out=warm[:], in_=warm[:], func=ACTF.Exp)
+
+        e_sb = [const.tile([P, 4, P], BF16, name="e_sb%d" % t) for t in range(NT)]
+
+        def zero_e(t):
+            nc.vector.memset(e_sb[t][:].rearrange("p t c -> p (t c)").bitcast(I32), 0)
+
+        for t in range(16):
+            zero_e(t)
+        mask_b = const.tile([P, 4, 4, 8], BF16, name="mask_b")
+        for kind in (K_FIRST, K_LAST):
+            nc.vector.tensor_copy(
+                out=mask_b[:, kind], in_=mask_f[:, kind, :].rearrange("p (g t) -> p t g", t=4)
+            )
+        nc.vector.memset(mask_b[:, K_SINK], NEG)
+        nc.vector.memset(mask_b[:, K_SINK, :, 0:1], 0.0)
+        nc.vector.tensor_copy(out=mask_b[:, K_FIRST8], in_=mask_b[:, K_FIRST])
+        nc.vector.memset(mask_b[:, K_FIRST8, :, 0:1], 0.0)
+        for t in range(16, NT):
+            zero_e(t)
+
+        v_grp = [const.tile([P, B, D, 4], BF16, name="v_grp%d" % o, align_bytes=64) for o in range(5)]
+        v_cod = [const.tile([P, B * D], U32, name="v_cod%d" % o, align_bytes=64) for o in range(5)]
+        v_scl = [const.tile([P, B * D], U8, name="v_scl%d" % o, align_bytes=64) for o in range(5)]
+        for o in range(5):
+            nc.gpsimd.tensor_scalar(
+                out=v_grp[o][:],
+                in0=v_raw[o][:].rearrange("p b (t d) -> p b d t", t=4),
+                scalar1=1.0, scalar2=0.0, op0=ALU.mult, op1=ALU.add,
+            )
+
+        def quant_v(o):
+            nc.vector.quantize_mx(
+                out=v_cod[o][:].bitcast(FP8X4),
+                scales=v_scl[o][:],
+                in_=v_grp[o][:].rearrange("p b d t -> p (b d t)"),
+            )
+
+        kT = [const.tile([P, 4, S // 4], BF16, name="kT%d" % b) for b in range(B)]
+        qT = {}
+
+        def k_first():
+            kps = ps_t.tile([P, 8, P], BF16, name="kps", tag="tp")
+            for a in range(8):
+                nc.tensor.transpose(kps[:, a, :], k_sb[0][:, a, :], ident[:])
+            nc.scalar.copy(
+                out=kT[0][:],
+                in_=kps[:].rearrange("p a c -> p (a c)").rearrange("p (g t) -> p t g", t=4),
+            )
+
+        aux_ps = {}
+
+        def aux_pe(j, kb, kx):
+            aps = ps_a.tile([P, 4, P], BF16, name="aps", tag="aps")
+            aux_ps[j] = aps
+            if j < PAIRS:
+                for n in range(2):
+                    u = 2 * j + n
+                    nc.tensor.transpose(aps[:, n, :], q_sb[u // 8][:, u % 8, :], ident[:])
+            if kb >= 1:
+                for n in range(2):
+                    nc.tensor.transpose(aps[:, 2 + n, :], k_sb[kb][:, 2 * kx + n, :], ident[:])
+
+        def aux_cp(j, kb, kx, eng):
+            aps = aux_ps[j]
+            if j < PAIRS:
+                qT[j] = qtp.tile([P, 2, P], BF16, name="qT", tag="qT")
+                if eng == "act":
+                    nc.scalar.copy(out=qT[j][:], in_=aps[:, 0:2, :])
+                else:
+                    nc.vector.tensor_copy(out=qT[j][:], in_=aps[:, 0:2, :])
+            if kb >= 1:
+                nc.vector.tensor_copy(
+                    out=kT[kb][:, :, 64 * kx : 64 * kx + 64],
+                    in_=aps[:, 2:4, :].rearrange("p a c -> p (a c)").rearrange("p (g t) -> p t g", t=4),
+                )
+
+        k_first()
+        for j in range(2):
+            aux_pe(j, 0, 0)
+            aux_cp(j, 0, 0, "act")
+
+        s_ps, mx, nb, rs, rc, tps, grp, cod, scl, o_ps, o_sb = {}, {}, {}, {}, {}, {}, {}, {}, {}, {}, {}
+
+        def ok(j):
+            return 0 <= j < PAIRS
+
+        def st_qk(j):
+            for n in range(2):
+                u = 2 * j + n
+                b, t = u // NT, u % NT
+                o, a, nsl, segs, bmasks = plan(t)
+                s = ps_s.tile([P, 4, 8 * RUN], F32, name="s", tag="s")
+                s_ps[u] = s
+                lhs = qT[j][:, n, :]
+                ops = []
+                for idx, kb, cnt in segs:
+                    ops.append((s[:, :, 8 * idx : 8 * (idx + cnt)], lhs, kT[b][:, :, 8 * kb : 8 * (kb + cnt)]))
+                for idx, kind in bmasks:
+                    ops.append((s[:, :, 8 * idx : 8 * idx + 8], ident[:], mask_b[:, kind]))
+                for i, (o_ap, l_ap, r_ap) in enumerate(ops):
+                    nc.tensor.matmul(out=o_ap, lhsT=l_ap, rhs=r_ap, start=(i == 0), stop=(i == len(ops) - 1))
+
+        def st_max(j):
+            mx[j] = small.tile([P, 2], F32, name="mx", tag="mx")
+            for n in range(2):
+                u = 2 * j + n
+                nsl = plan(u % NT)[2]
+                nc.vector.tensor_reduce(out=mx[j][:, n : n + 1], in_=s_ps[u][:, :, 0 : 8 * nsl], axis=AX.XY, op=ALU.max)
+
+        def st_nb(j):
+            nb[j] = small.tile([P, 2], F32, name="nb", tag="nb")
+            nc.vector.tensor_scalar(out=nb[j][:], in0=mx[j][:], scalar1=-SCALE, scalar2=None, op0=ALU.mult)
+
+        def st_exp(j):
+            rs[j] = small.tile([P, 2], F32, name="rs", tag="rs")
+            for n in range(2):
+                u = 2 * j + n
+                t = u % NT
+                o, a, nsl, segs, bmasks = plan(t)
+                nc.scalar.activation(
+                    out=e_sb[t][:, :, 8 * a : 8 * (a + nsl)],
+                    in_=s_ps[u][:, :, 0 : 8 * nsl],
+                    func=ACTF.Exp, bias=nb[j][:, n : n + 1], scale=SCALE,
+                    accum_out=rs[j][:, n : n + 1],
+                )
+
+        def st_tr(j):
+            tps[j] = ps_t.tile([P, 2, 4, P], BF16, name="tps", tag="tp")
+            for n in range(2):
+                t = (2 * j + n) % NT
+                for w in range(4):
+                    nc.tensor.transpose(tps[j][:, n, w, :], e_sb[t][:, w, :], ident[:])
+
+        def st_regroup(j):
+            grp[j] = grpp.tile([P, 2, P, 4], BF16, name="grp", tag="grp", align_bytes=64)
+            src = tps[j][:].rearrange("p n w r -> p n r w")
+            if j % RG_V_EVERY == RG_V_EVERY - 1:
+                nc.vector.tensor_copy(out=grp[j][:], in_=src)
+            else:
+                nc.scalar.copy(out=grp[j][:], in_=src)
+
+        def st_quant(j):
+            cod[j] = codp.tile([P, 2 * P], U32, name="cod", tag="cod", align_bytes=64)
+            scl[j] = codp.tile([P, 2 * P], U8, name="scl", tag="scl", align_bytes=64)
+            nc.vector.quantize_mx(
+                out=cod[j][:].bitcast(FP8X4), scales=scl[j][:],
+                in_=grp[j][:].rearrange("p n r w -> p (n r w)"),
+            )
+
+        def st_mx(j):
+            o_ps[j] = ps_o.tile([P, 2, D], F32, name="o_ps", tag="o_ps")
+            for n in range(2):
+                u = 2 * j + n
+                b, t = u // NT, u % NT
+                o = plan(t)[0]
+                nc.tensor.matmul_mx(
+                    out=o_ps[j][:, n, :],
+                    lhsT=cod[j][:, P * n : P * (n + 1)].bitcast(FP8X4),
+                    lhsT_scale=scl[j][:, P * n : P * (n + 1)],
+                    rhs=v_cod[o][:, D * b : D * (b + 1)].bitcast(FP8X4),
+                    rhs_scale=v_scl[o][:, D * b : D * (b + 1)],
+                    start=True, stop=True,
+                )
+
+        def st_rc(j):
+            rc[j] = small.tile([P, 2], F32, name="rc", tag="rc")
+            nc.vector.reciprocal(out=rc[j][:], in_=rs[j][:])
+
+        def st_norm(j):
+            m, h = j // 2, j % 2
+            if h == 0:
+                o_sb[m] = osbp.tile([P, 4, D], F32, name="o_sb", tag="o_sb")
+            nc.vector.tensor_tensor(
+                out=o_sb[m][:, 2 * h : 2 * h + 2, :], in0=o_ps[j][:],
+                in1=rc[j][:].unsqueeze(2).to_broadcast([P, 2, D]), op=ALU.mult,
+            )
+            if h == 1:
+                nc.sync.dma_start(out=o_view[:, 4 * m : 4 * m + 4, :], in_=o_sb[m][:])
+
+        V_QUANT_AT = {1: 0, 4: 1, 7: 2, 10: 3, 13: 4}
+
+        for i in range(-1, PAIRS + 4):
+            kb, kx = (i + 8) // 16, (i + 8) % 16
+            if not (1 <= kb < B and kx < 4):
+                kb, kx = 0, 0
+            has_aux = i + 3 < PAIRS or kb >= 1
+            if has_aux:
+                aux_pe(i + 3, kb, kx)
+                aux_cp(i + 3, kb, kx, "dve")
+            if ok(i - 4):
+                st_norm(i - 4)
+            if ok(i - 1):
+                st_tr(i - 1)
+            if ok(i + 1):
+                st_qk(i + 1)
+            if ok(i - 3):
+                st_mx(i - 3)
+            if ok(i):
+                st_exp(i)
+            rg_v = ok(i - 1) and (i - 1) % RG_V_EVERY == RG_V_EVERY - 1
+            if ok(i - 1) and not rg_v:
+                st_regroup(i - 1)
+            if ok(i + 1):
+                st_max(i + 1)
+            if ok(i - 3):
+                st_rc(i - 3)
+            if ok(i + 1):
+                st_nb(i + 1)
+            if i in V_QUANT_AT:
+                quant_v(V_QUANT_AT[i])
+            if ok(i - 2):
+                st_quant(i - 2)
+            if rg_v:
+                st_regroup(i - 1)

@@ -21,6 +21,7 @@ POS = P // H
 NT = S // POS
 UNITS = B * NT
 PAIRS = UNITS // 2
+QUADS = UNITS // 4
 RUN = 10
 SCALE = 1.0 / math.sqrt(D)
 NEG = -1.0e30
@@ -32,7 +33,7 @@ OPER = [list(range(16))] + [
     list(range(c, c + 8)) + [0] + list(range(c + 8, c + 15)) for c in BASES
 ]
 K_FIRST, K_LAST, K_SINK, K_FIRST8 = 0, 1, 2, 3
-RG_V_EVERY = 1000
+E_TILES = 18
 
 
 def plan(t):
@@ -65,15 +66,23 @@ def plan(t):
     return o, a, n, segs, bmasks
 
 
+def e_index(t):
+    if t <= 9:
+        return 7 + t
+    if t == NT - 1:
+        return 17
+    return plan(t)[1]
+
+
 def tile_swa_sinkmeta_t_kernel(tc, query_states, key_states, value_states, out):
     nc = tc.nc
     with ExitStack() as ctx:
         ctx.enter_context(tc.manual_schedule())
         const = ctx.enter_context(tc.tile_pool(name="const", bufs=1))
-        qtp = ctx.enter_context(tc.tile_pool(name="qtp", bufs=5))
+        qtp = ctx.enter_context(tc.tile_pool(name="qtp", bufs=4))
         grpp = ctx.enter_context(tc.tile_pool(name="grpp", bufs=3))
         codp = ctx.enter_context(tc.tile_pool(name="codp", bufs=3))
-        osbp = ctx.enter_context(tc.tile_pool(name="osbp", bufs=8))
+        osbp = ctx.enter_context(tc.tile_pool(name="osbp", bufs=6))
         small = ctx.enter_context(tc.tile_pool(name="small", bufs=8))
         ps_s = ctx.enter_context(tc.psum_pool(name="ps_s", bufs=4))
         ps_t = ctx.enter_context(tc.psum_pool(name="ps_t", bufs=2))
@@ -125,6 +134,8 @@ def tile_swa_sinkmeta_t_kernel(tc, query_states, key_states, value_states, out):
 
         ident = const.tile([P, P], BF16, name="ident")
         make_identity(nc, ident[:])
+        ident_f = const.tile([P, P], F32, name="ident_f")
+        make_identity(nc, ident_f[:])
         mask_f = const.tile([P, 2, BLK], F32, name="mask_f")
         nc.gpsimd.memset(mask_f[:], 0.0)
         nc.gpsimd.affine_select(
@@ -140,43 +151,44 @@ def tile_swa_sinkmeta_t_kernel(tc, query_states, key_states, value_states, out):
         nc.vector.memset(warm[:], 0.0)
         nc.scalar.activation(out=warm[:], in_=warm[:], func=ACTF.Exp)
 
-        e_sb = [const.tile([P, 4, P], BF16, name="e_sb%d" % t) for t in range(NT)]
+        e_all = const.tile([P, E_TILES, 2, 2 * P], BF16, name="e_all")
 
-        def zero_e(t):
-            nc.vector.memset(e_sb[t][:].rearrange("p t c -> p (t c)").bitcast(I32), 0)
+        def zero_e(lo, hi):
+            nc.vector.memset(e_all[:, lo:hi].rearrange("p k u c -> p (k u c)").bitcast(I32), 0)
 
-        for t in range(16):
-            zero_e(t)
-        mask_b = const.tile([P, 4, 4, 8], BF16, name="mask_b")
+        zero_e(7, 12)
+        mask_b = const.tile([P, 4, 2, 16], BF16, name="mask_b")
         for kind in (K_FIRST, K_LAST):
             nc.vector.tensor_copy(
-                out=mask_b[:, kind], in_=mask_f[:, kind, :].rearrange("p (g t) -> p t g", t=4)
+                out=mask_b[:, kind].rearrange("p u (g e) -> p u g e", e=2),
+                in_=mask_f[:, kind, :].rearrange("p (g u e) -> p u g e", u=2, e=2),
             )
         nc.vector.memset(mask_b[:, K_SINK], NEG)
-        nc.vector.memset(mask_b[:, K_SINK, :, 0:1], 0.0)
+        nc.vector.memset(mask_b[:, K_SINK, :, 0:2], 0.0)
         nc.vector.tensor_copy(out=mask_b[:, K_FIRST8], in_=mask_b[:, K_FIRST])
-        nc.vector.memset(mask_b[:, K_FIRST8, :, 0:1], 0.0)
-        for t in range(16, NT):
-            zero_e(t)
+        nc.vector.memset(mask_b[:, K_FIRST8, :, 0:2], 0.0)
+        zero_e(12, E_TILES)
+        zero_e(0, 7)
 
         v_grp = [const.tile([P, B, D, 4], BF16, name="v_grp%d" % o, align_bytes=64) for o in range(5)]
         v_cod = [const.tile([P, B * D], U32, name="v_cod%d" % o, align_bytes=64) for o in range(5)]
         v_scl = [const.tile([P, B * D], U8, name="v_scl%d" % o, align_bytes=64) for o in range(5)]
-        for o in range(5):
+
+        def regroup_v(o, b):
             nc.gpsimd.tensor_scalar(
-                out=v_grp[o][:],
-                in0=v_raw[o][:].rearrange("p b (t d) -> p b d t", t=4),
+                out=v_grp[o][:, b],
+                in0=v_raw[o][:, b].rearrange("p (t d) -> p d t", t=4),
                 scalar1=1.0, scalar2=0.0, op0=ALU.mult, op1=ALU.add,
             )
 
-        def quant_v(o):
+        def quant_v(o, b):
             nc.vector.quantize_mx(
-                out=v_cod[o][:].bitcast(FP8X4),
-                scales=v_scl[o][:],
-                in_=v_grp[o][:].rearrange("p b d t -> p (b d t)"),
+                out=v_cod[o][:, D * b : D * (b + 1)].bitcast(FP8X4),
+                scales=v_scl[o][:, D * b : D * (b + 1)],
+                in_=v_grp[o][:, b].rearrange("p d t -> p (d t)"),
             )
 
-        kT = [const.tile([P, 4, S // 4], BF16, name="kT%d" % b) for b in range(B)]
+        kT = [const.tile([P, 2, S // 2], BF16, name="kT%d" % b) for b in range(B)]
         qT = {}
 
         def k_first():
@@ -184,41 +196,37 @@ def tile_swa_sinkmeta_t_kernel(tc, query_states, key_states, value_states, out):
             for a in range(8):
                 nc.tensor.transpose(kps[:, a, :], k_sb[0][:, a, :], ident[:])
             nc.scalar.copy(
-                out=kT[0][:],
-                in_=kps[:].rearrange("p a c -> p (a c)").rearrange("p (g t) -> p t g", t=4),
+                out=kT[0][:].rearrange("p u (g e) -> p u g e", e=2),
+                in_=kps[:].rearrange("p a c -> p (a c)").rearrange("p (g u e) -> p u g e", u=2, e=2),
             )
 
         aux_ps = {}
 
-        def aux_pe(j, kb, kx):
-            aps = ps_a.tile([P, 4, P], BF16, name="aps", tag="aps")
-            aux_ps[j] = aps
-            if j < PAIRS:
-                for n in range(2):
-                    u = 2 * j + n
+        def aux_pe(m, kb, kh):
+            aps = ps_a.tile([P, 8, P], BF16, name="aps", tag="aps")
+            aux_ps[m] = aps
+            if m < QUADS:
+                for n in range(4):
+                    u = 4 * m + n
                     nc.tensor.transpose(aps[:, n, :], q_sb[u // 8][:, u % 8, :], ident[:])
             if kb >= 1:
-                for n in range(2):
-                    nc.tensor.transpose(aps[:, 2 + n, :], k_sb[kb][:, 2 * kx + n, :], ident[:])
+                for n in range(4):
+                    nc.tensor.transpose(aps[:, 4 + n, :], k_sb[kb][:, 4 * kh + n, :], ident[:])
 
-        def aux_cp(j, kb, kx, eng):
-            aps = aux_ps[j]
-            if j < PAIRS:
-                qT[j] = qtp.tile([P, 2, P], BF16, name="qT", tag="qT")
-                if eng == "act":
-                    nc.scalar.copy(out=qT[j][:], in_=aps[:, 0:2, :])
-                else:
-                    nc.vector.tensor_copy(out=qT[j][:], in_=aps[:, 0:2, :])
+        def aux_cp(m, kb, kh):
+            aps = aux_ps[m]
+            if m < QUADS:
+                qT[m] = qtp.tile([P, 4, P], BF16, name="qT", tag="qT")
+                nc.scalar.copy(out=qT[m][:], in_=aps[:, 0:4, :])
             if kb >= 1:
                 nc.vector.tensor_copy(
-                    out=kT[kb][:, :, 64 * kx : 64 * kx + 64],
-                    in_=aps[:, 2:4, :].rearrange("p a c -> p (a c)").rearrange("p (g t) -> p t g", t=4),
+                    out=kT[kb][:, :, 256 * kh : 256 * kh + 256].rearrange("p u (g e) -> p u g e", e=2),
+                    in_=aps[:, 4:8, :].rearrange("p a c -> p (a c)").rearrange("p (g u e) -> p u g e", u=2, e=2),
                 )
 
         k_first()
-        for j in range(2):
-            aux_pe(j, 0, 0)
-            aux_cp(j, 0, 0, "act")
+        aux_pe(0, 0, 0)
+        aux_cp(0, 0, 0)
 
         s_ps, mx, nb, rs, rc, tps, grp, cod, scl, o_ps, o_sb = {}, {}, {}, {}, {}, {}, {}, {}, {}, {}, {}
 
@@ -230,62 +238,62 @@ def tile_swa_sinkmeta_t_kernel(tc, query_states, key_states, value_states, out):
                 u = 2 * j + n
                 b, t = u // NT, u % NT
                 o, a, nsl, segs, bmasks = plan(t)
-                s = ps_s.tile([P, 4, 8 * RUN], F32, name="s", tag="s")
+                s = ps_s.tile([P, 2, 16 * RUN], F32, name="s", tag="s")
                 s_ps[u] = s
-                lhs = qT[j][:, n, :]
+                lhs = qT[j // 2][:, 2 * (j % 2) + n, :]
                 ops = []
                 for idx, kb, cnt in segs:
-                    ops.append((s[:, :, 8 * idx : 8 * (idx + cnt)], lhs, kT[b][:, :, 8 * kb : 8 * (kb + cnt)]))
+                    ops.append((s[:, :, 16 * idx : 16 * (idx + cnt)], lhs, kT[b][:, :, 16 * kb : 16 * (kb + cnt)]))
                 for idx, kind in bmasks:
-                    ops.append((s[:, :, 8 * idx : 8 * idx + 8], ident[:], mask_b[:, kind]))
+                    ops.append((s[:, :, 16 * idx : 16 * idx + 16], ident[:], mask_b[:, kind]))
                 for i, (o_ap, l_ap, r_ap) in enumerate(ops):
                     nc.tensor.matmul(out=o_ap, lhsT=l_ap, rhs=r_ap, start=(i == 0), stop=(i == len(ops) - 1))
 
         def st_max(j):
             mx[j] = small.tile([P, 2], F32, name="mx", tag="mx")
+            nb[j] = small.tile([P, 2], F32, name="nb", tag="nb")
             for n in range(2):
                 u = 2 * j + n
                 nsl = plan(u % NT)[2]
-                nc.vector.tensor_reduce(out=mx[j][:, n : n + 1], in_=s_ps[u][:, :, 0 : 8 * nsl], axis=AX.XY, op=ALU.max)
-
-        def st_nb(j):
-            nb[j] = small.tile([P, 2], F32, name="nb", tag="nb")
-            nc.vector.tensor_scalar(out=nb[j][:], in0=mx[j][:], scalar1=-SCALE, scalar2=None, op0=ALU.mult)
+                nc.vector.tensor_reduce(out=mx[j][:, n : n + 1], in_=s_ps[u][:, :, 0 : 16 * nsl], axis=AX.XY, op=ALU.max)
+                nc.gpsimd.tensor_scalar(
+                    out=nb[j][:, n : n + 1], in0=mx[j][:, n : n + 1],
+                    scalar1=-SCALE, scalar2=0.0, op0=ALU.mult, op1=ALU.add,
+                )
 
         def st_exp(j):
-            rs[j] = small.tile([P, 2], F32, name="rs", tag="rs")
+            m, h = j // 2, j % 2
+            if h == 0:
+                rs[m] = small.tile([P, 4], F32, name="rs", tag="rs")
             for n in range(2):
                 u = 2 * j + n
                 t = u % NT
                 o, a, nsl, segs, bmasks = plan(t)
                 nc.scalar.activation(
-                    out=e_sb[t][:, :, 8 * a : 8 * (a + nsl)],
-                    in_=s_ps[u][:, :, 0 : 8 * nsl],
+                    out=e_all[:, e_index(t), :, 16 * a : 16 * (a + nsl)],
+                    in_=s_ps[u][:, :, 0 : 16 * nsl],
                     func=ACTF.Exp, bias=nb[j][:, n : n + 1], scale=SCALE,
-                    accum_out=rs[j][:, n : n + 1],
+                    accum_out=rs[m][:, 2 * h + n : 2 * h + n + 1],
                 )
 
         def st_tr(j):
-            tps[j] = ps_t.tile([P, 2, 4, P], BF16, name="tps", tag="tp")
+            tps[j] = ps_t.tile([P, 2, 2, P], F32, name="tps", tag="tp")
             for n in range(2):
                 t = (2 * j + n) % NT
-                for w in range(4):
-                    nc.tensor.transpose(tps[j][:, n, w, :], e_sb[t][:, w, :], ident[:])
+                words = e_all[:, e_index(t)].rearrange("p u c -> p (u c)").bitcast(F32)
+                for w in range(2):
+                    nc.tensor.transpose(tps[j][:, n, w, :], words[:, P * w : P * (w + 1)], ident_f[:])
 
         def st_regroup(j):
-            grp[j] = grpp.tile([P, 2, P, 4], BF16, name="grp", tag="grp", align_bytes=64)
-            src = tps[j][:].rearrange("p n w r -> p n r w")
-            if j % RG_V_EVERY == RG_V_EVERY - 1:
-                nc.vector.tensor_copy(out=grp[j][:], in_=src)
-            else:
-                nc.scalar.copy(out=grp[j][:], in_=src)
+            grp[j] = grpp.tile([P, 2, P, 2], F32, name="grp", tag="grp", align_bytes=64)
+            nc.scalar.copy(out=grp[j][:], in_=tps[j][:].rearrange("p n w r -> p n r w"))
 
         def st_quant(j):
             cod[j] = codp.tile([P, 2 * P], U32, name="cod", tag="cod", align_bytes=64)
             scl[j] = codp.tile([P, 2 * P], U8, name="scl", tag="scl", align_bytes=64)
             nc.vector.quantize_mx(
                 out=cod[j][:].bitcast(FP8X4), scales=scl[j][:],
-                in_=grp[j][:].rearrange("p n r w -> p (n r w)"),
+                in_=grp[j][:].rearrange("p n r w -> p (n r w)").bitcast(BF16),
             )
 
         def st_mx(j):
@@ -303,9 +311,9 @@ def tile_swa_sinkmeta_t_kernel(tc, query_states, key_states, value_states, out):
                     start=True, stop=True,
                 )
 
-        def st_rc(j):
-            rc[j] = small.tile([P, 2], F32, name="rc", tag="rc")
-            nc.vector.reciprocal(out=rc[j][:], in_=rs[j][:])
+        def st_rc(m):
+            rc[m] = small.tile([P, 4], F32, name="rc", tag="rc")
+            nc.vector.reciprocal(out=rc[m][:], in_=rs[m][:])
 
         def st_norm(j):
             m, h = j // 2, j % 2
@@ -313,43 +321,52 @@ def tile_swa_sinkmeta_t_kernel(tc, query_states, key_states, value_states, out):
                 o_sb[m] = osbp.tile([P, 4, D], F32, name="o_sb", tag="o_sb")
             nc.vector.tensor_tensor(
                 out=o_sb[m][:, 2 * h : 2 * h + 2, :], in0=o_ps[j][:],
-                in1=rc[j][:].unsqueeze(2).to_broadcast([P, 2, D]), op=ALU.mult,
+                in1=rc[m][:, 2 * h : 2 * h + 2].unsqueeze(2).to_broadcast([P, 2, D]), op=ALU.mult,
             )
             if h == 1:
                 nc.sync.dma_start(out=o_view[:, 4 * m : 4 * m + 4, :], in_=o_sb[m][:])
 
-        V_QUANT_AT = {1: 0, 4: 1, 7: 2, 10: 3, 13: 4}
+        FIRST_PAIR = (0, 5, 8, 12, 15)
+        v_regroup_at = {}
+        v_quant_at = {}
+        for b in range(B):
+            for o in range(5):
+                need = 16 * b + FIRST_PAIR[o] + 4
+                v_quant_at[need - 2] = (o, b)
+                v_regroup_at[need - 5] = (o, b)
 
-        for i in range(-1, PAIRS + 4):
-            kb, kx = (i + 8) // 16, (i + 8) % 16
-            if not (1 <= kb < B and kx < 4):
-                kb, kx = 0, 0
-            has_aux = i + 3 < PAIRS or kb >= 1
-            if has_aux:
-                aux_pe(i + 3, kb, kx)
-                aux_cp(i + 3, kb, kx, "dve")
-            if ok(i - 4):
-                st_norm(i - 4)
-            if ok(i - 1):
-                st_tr(i - 1)
+        for i in range(-2, PAIRS + 6):
             if ok(i + 1):
                 st_qk(i + 1)
-            if ok(i - 3):
-                st_mx(i - 3)
+            kb, kh = 0, 0
+            if i % 2 == 0:
+                if i % 16 in (8, 10) and i // 16 + 1 < B:
+                    kb, kh = i // 16 + 1, (i % 16 - 8) // 2
+                if (i + 4) // 2 < QUADS or kb >= 1:
+                    aux_pe((i + 4) // 2, kb, kh)
+            if ok(i - 1):
+                st_tr(i - 1)
+            if ok(i - 2):
+                st_regroup(i - 2)
+            if i % 2 == 1:
+                ip = i - 1
+                if ip % 16 in (8, 10) and ip // 16 + 1 < B:
+                    kb, kh = ip // 16 + 1, (ip % 16 - 8) // 2
+                if (ip + 4) // 2 < QUADS or kb >= 1:
+                    aux_cp((ip + 4) // 2, kb, kh)
             if ok(i):
                 st_exp(i)
-            rg_v = ok(i - 1) and (i - 1) % RG_V_EVERY == RG_V_EVERY - 1
-            if ok(i - 1) and not rg_v:
-                st_regroup(i - 1)
+            if ok(i - 3):
+                st_quant(i - 3)
+            if ok(i - 5):
+                st_norm(i - 5)
+            if ok(i - 4):
+                st_mx(i - 4)
             if ok(i + 1):
                 st_max(i + 1)
-            if ok(i - 3):
-                st_rc(i - 3)
-            if ok(i + 1):
-                st_nb(i + 1)
-            if i in V_QUANT_AT:
-                quant_v(V_QUANT_AT[i])
-            if ok(i - 2):
-                st_quant(i - 2)
-            if rg_v:
-                st_regroup(i - 1)
+            if i % 2 == 1 and ok(i - 2):
+                st_rc((i - 2) // 2)
+            if i in v_quant_at:
+                quant_v(v_quant_at[i][0], v_quant_at[i][1])
+            if i in v_regroup_at:
+                regroup_v(v_regroup_at[i][0], v_regroup_at[i][1])

@@ -28,50 +28,33 @@ NEG = -1.0e30
 ALLOWED = sum(min(i, WIN) + 1 + min(max(i - WIN, 0), META) for i in range(S))
 FLOPS = 4 * D * ALLOWED * B * H
 
-BASES = (2, 9, 16, 17)
-OPER = [list(range(16))] + [
-    list(range(c, c + 8)) + [0] + list(range(c + 8, c + 15)) for c in BASES
-]
-K_FIRST, K_LAST, K_SINK, K_FIRST8 = 0, 1, 2, 3
-E_TILES = 18
+E_SLOTS = 35
+SINK_SLOTS = (8, 17, 26)
+WINDOWS = (0, 7, 14, 19)
+K_FIRST, K_LAST, K_SINK, K_FIRST8, K_NONE = 0, 1, 2, 3, 4
+E_TILES = 15
+
+
+def eslot(block):
+    return block + block // 8
+
+
+def eblock(slot):
+    return 0 if slot in SINK_SLOTS else slot - slot // 9
 
 
 def plan(t):
-    if t <= 9:
-        o, a, n = 0, 0, min(t, 9) + 1
-    elif t <= 16:
-        o, a, n = 1, t - 10, RUN
-    elif t <= 23:
-        o, a, n = 2, t - 17, RUN
-    elif t <= 30:
-        o, a, n = 3, t - 24, RUN
+    if t < 8:
+        start, n, sink = 0, t + 1, None
     else:
-        o, a, n = 4, 6, RUN
-    slots = OPER[o][a : a + n]
-    segs = []
-    bmasks = []
-    for idx, kb in enumerate(slots):
-        if segs and kb == segs[-1][1] + segs[-1][2]:
-            segs[-1][2] += 1
-        else:
-            segs.append([idx, kb, 1])
-        if kb == t:
-            bmasks.append((idx, K_LAST))
-        elif kb == t - 8:
-            bmasks.append((idx, K_FIRST8 if kb == 0 else K_FIRST))
-        elif kb == 0 and t > 8:
-            bmasks.append((idx, K_SINK))
-        else:
-            assert t - 8 < kb < t
-    return o, a, n, segs, bmasks
+        start, n = eslot(t - 8), RUN
+        sink = [x for x in SINK_SLOTS if start < x < start + n][0] - start
+    o = min(start // 7, 3)
+    return start, n, o, start - WINDOWS[o], sink
 
 
 def e_index(t):
-    if t <= 9:
-        return 7 + t
-    if t == NT - 1:
-        return 17
-    return plan(t)[1]
+    return plan(t)[3] if t >= 8 else 7 + t
 
 
 def tile_swa_sinkmeta_t_kernel(tc, query_states, key_states, value_states, out):
@@ -100,7 +83,7 @@ def tile_swa_sinkmeta_t_kernel(tc, query_states, key_states, value_states, out):
 
         k_sb = [const.tile([P, 8, D], BF16, name="k_sb%d" % b) for b in range(B)]
         q_sb = [const.tile([P, 8, D], BF16, name="q_sb%d" % c) for c in range(UNITS // 8)]
-        v_raw = [const.tile([P, B, 4 * D], BF16, name="v_raw%d" % o) for o in range(5)]
+        v_raw = [const.tile([P, B, 4 * D], BF16, name="v_raw%d" % o) for o in range(4)]
 
         def load_k(b):
             nc.sync.dma_start(out=k_sb[b][:], in_=k_view[:, 8 * b : 8 * b + 8, :])
@@ -109,13 +92,15 @@ def tile_swa_sinkmeta_t_kernel(tc, query_states, key_states, value_states, out):
             nc.sync.dma_start(out=q_sb[c][:], in_=q_view[:, 8 * c : 8 * c + 8, :])
 
         def load_v(o):
-            if o == 0:
-                nc.sync.dma_start(out=v_raw[0][:], in_=v_rows(0, 512))
-            else:
-                c = BASES[o - 1]
-                nc.sync.dma_start(out=v_raw[o][0:64], in_=v_rows(BLK * c, 256))
-                nc.sync.dma_start(out=v_raw[o][64:72], in_=v_rows(0, BLK))
-                nc.sync.dma_start(out=v_raw[o][72:128], in_=v_rows(BLK * (c + 8), 224))
+            x = 0
+            while x < 16:
+                y = x + 1
+                while y < 16 and eblock(WINDOWS[o] + y) == eblock(WINDOWS[o] + y - 1) + 1:
+                    y += 1
+                nc.sync.dma_start(
+                    out=v_raw[o][8 * x : 8 * y], in_=v_rows(BLK * eblock(WINDOWS[o] + x), BLK * (y - x))
+                )
+                x = y
 
         load_k(0)
         load_q(0)
@@ -126,7 +111,6 @@ def tile_swa_sinkmeta_t_kernel(tc, query_states, key_states, value_states, out):
         load_v(2)
         load_q(3)
         load_v(3)
-        load_v(4)
         for b in range(1, B):
             load_k(b)
             for c in range(4 * b, 4 * b + 4):
@@ -157,7 +141,7 @@ def tile_swa_sinkmeta_t_kernel(tc, query_states, key_states, value_states, out):
             nc.vector.memset(e_all[:, lo:hi].rearrange("p k u c -> p (k u c)").bitcast(I32), 0)
 
         zero_e(7, 12)
-        mask_b = const.tile([P, 4, 2, 16], BF16, name="mask_b")
+        mask_b = const.tile([P, 5, 2, 16], BF16, name="mask_b")
         for kind in (K_FIRST, K_LAST):
             nc.vector.tensor_copy(
                 out=mask_b[:, kind].rearrange("p u (g e) -> p u g e", e=2),
@@ -167,12 +151,17 @@ def tile_swa_sinkmeta_t_kernel(tc, query_states, key_states, value_states, out):
         nc.vector.memset(mask_b[:, K_SINK, :, 0:2], 0.0)
         nc.vector.tensor_copy(out=mask_b[:, K_FIRST8], in_=mask_b[:, K_FIRST])
         nc.vector.memset(mask_b[:, K_FIRST8, :, 0:2], 0.0)
+        nc.vector.memset(mask_b[:, K_NONE], NEG)
+        mask_fl = const.tile([P, 2, 2, 2, 16], BF16, name="mask_fl")
+        for w, kind in ((0, K_FIRST), (1, K_FIRST8)):
+            nc.vector.tensor_copy(out=mask_fl[:, w, :, 0, :], in_=mask_b[:, kind])
+            nc.vector.tensor_copy(out=mask_fl[:, w, :, 1, :], in_=mask_b[:, K_LAST])
         zero_e(12, E_TILES)
         zero_e(0, 7)
 
-        v_grp = [const.tile([P, B, D, 4], BF16, name="v_grp%d" % o, align_bytes=64) for o in range(5)]
-        v_cod = [const.tile([P, B * D], U32, name="v_cod%d" % o, align_bytes=64) for o in range(5)]
-        v_scl = [const.tile([P, B * D], U8, name="v_scl%d" % o, align_bytes=64) for o in range(5)]
+        v_grp = [const.tile([P, B, D, 4], BF16, name="v_grp%d" % o, align_bytes=64) for o in range(4)]
+        v_cod = [const.tile([P, B * D], U32, name="v_cod%d" % o, align_bytes=64) for o in range(4)]
+        v_scl = [const.tile([P, B * D], U8, name="v_scl%d" % o, align_bytes=64) for o in range(4)]
 
         def regroup_v(o, b):
             nc.gpsimd.tensor_scalar(
@@ -188,17 +177,32 @@ def tile_swa_sinkmeta_t_kernel(tc, query_states, key_states, value_states, out):
                 in_=v_grp[o][:, b].rearrange("p d t -> p (d t)"),
             )
 
-        kT = [const.tile([P, 2, S // 2], BF16, name="kT%d" % b) for b in range(B)]
+        kT = [const.tile([P, 2, 16 * (E_SLOTS + 1)], BF16, name="kT%d" % b) for b in range(B)]
         qT = {}
 
-        def k_first():
-            kps = ps_t.tile([P, 8, P], BF16, name="kps", tag="tp")
-            for a in range(8):
-                nc.tensor.transpose(kps[:, a, :], k_sb[0][:, a, :], ident[:])
-            nc.scalar.copy(
-                out=kT[0][:].rearrange("p u (g e) -> p u g e", e=2),
-                in_=kps[:].rearrange("p a c -> p (a c)").rearrange("p (g u e) -> p u g e", u=2, e=2),
+        def k_copy(eng, b, grp8, src):
+            dst = kT[b][:, :, 144 * grp8 : 144 * grp8 + 128].rearrange("p u (g e) -> p u g e", e=2)
+            view = src.rearrange("p a c -> p (a c)").rearrange("p (g u e) -> p u g e", u=2, e=2)
+            if eng == "act":
+                nc.scalar.copy(out=dst, in_=view)
+            else:
+                nc.vector.tensor_copy(out=dst, in_=view)
+
+        def k_sinks(b):
+            nc.gpsimd.tensor_scalar(
+                out=kT[b][:].rearrange("p u (x c) -> p u x c", c=16)[:, :, 8:27:9, :],
+                in0=kT[b][:, :, 0:16].unsqueeze(2).to_broadcast([P, 2, 3, 16]),
+                scalar1=1.0, scalar2=0.0, op0=ALU.mult, op1=ALU.add,
             )
+
+        def k_first():
+            for half, eng in ((0, "act"), (1, "dve")):
+                kps = ps_t.tile([P, 4, P], BF16, name="kps", tag="tp")
+                for a in range(4):
+                    nc.tensor.transpose(kps[:, a, :], k_sb[0][:, 4 * half + a, :], ident[:])
+                for g in range(2):
+                    k_copy(eng, 0, 2 * half + g, kps[:, 2 * g : 2 * g + 2, :])
+            k_sinks(0)
 
         aux_ps = {}
 
@@ -219,10 +223,10 @@ def tile_swa_sinkmeta_t_kernel(tc, query_states, key_states, value_states, out):
                 qT[m] = qtp.tile([P, 4, P], BF16, name="qT", tag="qT")
                 nc.scalar.copy(out=qT[m][:], in_=aps[:, 0:4, :])
             if kb >= 1:
-                nc.vector.tensor_copy(
-                    out=kT[kb][:, :, 256 * kh : 256 * kh + 256].rearrange("p u (g e) -> p u g e", e=2),
-                    in_=aps[:, 4:8, :].rearrange("p a c -> p (a c)").rearrange("p (g u e) -> p u g e", u=2, e=2),
-                )
+                for g in range(2):
+                    k_copy("dve", kb, 2 * kh + g, aps[:, 4 + 2 * g : 6 + 2 * g, :])
+                if kh == 0:
+                    k_sinks(kb)
 
         k_first()
         aux_pe(0, 0, 0)
@@ -237,15 +241,16 @@ def tile_swa_sinkmeta_t_kernel(tc, query_states, key_states, value_states, out):
             for n in range(2):
                 u = 2 * j + n
                 b, t = u // NT, u % NT
-                o, a, nsl, segs, bmasks = plan(t)
+                start, nsl, o, a, sink = plan(t)
                 s = ps_s.tile([P, 2, 16 * RUN], F32, name="s", tag="s")
                 s_ps[u] = s
-                lhs = qT[j // 2][:, 2 * (j % 2) + n, :]
-                ops = []
-                for idx, kb, cnt in segs:
-                    ops.append((s[:, :, 16 * idx : 16 * (idx + cnt)], lhs, kT[b][:, :, 16 * kb : 16 * (kb + cnt)]))
-                for idx, kind in bmasks:
-                    ops.append((s[:, :, 16 * idx : 16 * idx + 16], ident[:], mask_b[:, kind]))
+                slots = s[:].rearrange("p u (x c) -> p u x c", c=16)
+                ops = [(s[:, :, 0 : 16 * nsl], qT[j // 2][:, 2 * (j % 2) + n, :], kT[b][:, :, 16 * start : 16 * (start + nsl)])]
+                if t < 8:
+                    ops.append((s[:, :, 16 * t : 16 * t + 16], ident[:], mask_b[:, K_LAST]))
+                else:
+                    ops.append((slots[:, :, 0:RUN:RUN - 1, :], ident[:], mask_fl[:, 1 if t == 8 else 0]))
+                    ops.append((s[:, :, 16 * sink : 16 * sink + 16], ident[:], mask_b[:, K_NONE if t == 8 else K_SINK]))
                 for i, (o_ap, l_ap, r_ap) in enumerate(ops):
                     nc.tensor.matmul(out=o_ap, lhsT=l_ap, rhs=r_ap, start=(i == 0), stop=(i == len(ops) - 1))
 
@@ -254,7 +259,7 @@ def tile_swa_sinkmeta_t_kernel(tc, query_states, key_states, value_states, out):
             nb[j] = small.tile([P, 2], F32, name="nb", tag="nb")
             for n in range(2):
                 u = 2 * j + n
-                nsl = plan(u % NT)[2]
+                nsl = plan(u % NT)[1]
                 nc.vector.tensor_reduce(out=mx[j][:, n : n + 1], in_=s_ps[u][:, :, 0 : 16 * nsl], axis=AX.XY, op=ALU.max)
                 nc.gpsimd.tensor_scalar(
                     out=nb[j][:, n : n + 1], in0=mx[j][:, n : n + 1],
@@ -268,7 +273,7 @@ def tile_swa_sinkmeta_t_kernel(tc, query_states, key_states, value_states, out):
             for n in range(2):
                 u = 2 * j + n
                 t = u % NT
-                o, a, nsl, segs, bmasks = plan(t)
+                start, nsl, o, a, sink = plan(t)
                 nc.scalar.activation(
                     out=e_all[:, e_index(t), :, 16 * a : 16 * (a + nsl)],
                     in_=s_ps[u][:, :, 0 : 16 * nsl],
@@ -301,7 +306,7 @@ def tile_swa_sinkmeta_t_kernel(tc, query_states, key_states, value_states, out):
             for n in range(2):
                 u = 2 * j + n
                 b, t = u // NT, u % NT
-                o = plan(t)[0]
+                o = plan(t)[2]
                 nc.tensor.matmul_mx(
                     out=o_ps[j][:, n, :],
                     lhsT=cod[j][:, P * n : P * (n + 1)].bitcast(FP8X4),
@@ -326,11 +331,11 @@ def tile_swa_sinkmeta_t_kernel(tc, query_states, key_states, value_states, out):
             if h == 1:
                 nc.sync.dma_start(out=o_view[:, 4 * m : 4 * m + 4, :], in_=o_sb[m][:])
 
-        FIRST_PAIR = (0, 5, 8, 12, 15)
+        FIRST_PAIR = (0, 7, 10, 13)
         v_regroup_at = {}
         v_quant_at = {}
         for b in range(B):
-            for o in range(5):
+            for o in range(4):
                 need = 16 * b + FIRST_PAIR[o] + 4
                 v_quant_at[need - 2] = (o, b)
                 v_regroup_at[need - 5] = (o, b)

@@ -221,7 +221,7 @@ def tile_swa_sinkmeta_t_kernel(tc, query_states, key_states, value_states, out):
             aps = aux_ps[m]
             if m < QUADS:
                 qT[m] = qtp.tile([P, 4, P], BF16, name="qT", tag="qT")
-                nc.scalar.copy(out=qT[m][:], in_=aps[:, 0:4, :])
+                nc.vector.tensor_copy(out=qT[m][:], in_=aps[:, 0:4, :])
             if kb >= 1:
                 for g in range(2):
                     k_copy("dve", kb, 2 * kh + g, aps[:, 4 + 2 * g : 6 + 2 * g, :])

@@ -261,10 +261,7 @@ def tile_swa_sinkmeta_t_kernel(tc, query_states, key_states, value_states, out):
                 u = 2 * j + n
                 nsl = plan(u % NT)[1]
                 nc.vector.tensor_reduce(out=mx[j][:, n : n + 1], in_=s_ps[u][:, :, 0 : 16 * nsl], axis=AX.XY, op=ALU.max)
-                nc.gpsimd.tensor_scalar(
-                    out=nb[j][:, n : n + 1], in0=mx[j][:, n : n + 1],
-                    scalar1=-SCALE, scalar2=0.0, op0=ALU.mult, op1=ALU.add,
-                )
+            nc.scalar.activation(out=nb[j][:], in_=mx[j][:], func=ACTF.Copy, scale=-SCALE)
 
         def st_exp(j):
             m, h = j // 2, j % 2

@@ -57,6 +57,13 @@ def e_index(t):
     return plan(t)[3] if t >= 8 else 7 + t
 
 
+SEQ = [t for lead in range(8) for t in (lead, 8 + 3 * lead, 9 + 3 * lead, 10 + 3 * lead)]
+
+
+def unit_of(j, n):
+    return (2 * j + n) // NT, SEQ[(2 * j + n) % NT]
+
+
 def tile_swa_sinkmeta_t_kernel(tc, query_states, key_states, value_states, out):
     nc = tc.nc
     with ExitStack() as ctx:
@@ -69,8 +76,7 @@ def tile_swa_sinkmeta_t_kernel(tc, query_states, key_states, value_states, out):
         small = ctx.enter_context(tc.tile_pool(name="small", bufs=8))
         ps_s = ctx.enter_context(tc.psum_pool(name="ps_s", bufs=4))
         ps_t = ctx.enter_context(tc.psum_pool(name="ps_t", bufs=2))
-        ps_a = ctx.enter_context(tc.psum_pool(name="ps_a", bufs=1))
-        ps_o = ctx.enter_context(tc.psum_pool(name="ps_o", bufs=1))
+        ps_oa = ctx.enter_context(tc.psum_pool(name="ps_oa", bufs=1))
 
         q_view = query_states.rearrange("b s c -> (b s c)").rearrange(
             "(n r d) -> r n d", r=P, d=D
@@ -104,12 +110,12 @@ def tile_swa_sinkmeta_t_kernel(tc, query_states, key_states, value_states, out):
 
         load_k(0)
         load_q(0)
-        load_v(0)
         load_q(1)
-        load_v(1)
+        load_v(0)
         load_q(2)
-        load_v(2)
+        load_v(1)
         load_q(3)
+        load_v(2)
         load_v(3)
         for b in range(1, B):
             load_k(b)
@@ -204,43 +210,44 @@ def tile_swa_sinkmeta_t_kernel(tc, query_states, key_states, value_states, out):
                     k_copy(eng, 0, 2 * half + g, kps[:, 2 * g : 2 * g + 2, :])
             k_sinks(0)
 
-        aux_ps = {}
+        oa = [ps_oa.tile([P, 4 * P], F32, name="oa%d" % x) for x in range(2)]
 
-        def aux_pe(m, kb, kh):
-            aps = ps_a.tile([P, 8, P], BF16, name="aps", tag="aps")
-            aux_ps[m] = aps
-            if m < QUADS:
-                for n in range(4):
-                    u = 4 * m + n
-                    nc.tensor.transpose(aps[:, n, :], q_sb[u // 8][:, u % 8, :], ident[:])
-            if kb >= 1:
-                for n in range(4):
-                    nc.tensor.transpose(aps[:, 4 + n, :], k_sb[kb][:, 4 * kh + n, :], ident[:])
+        q_ps = oa[0][:, 2 * P : 4 * P].bitcast(BF16).rearrange("p (a c) -> p a c", c=P)
+        k_ps = oa[1][:, 2 * P : 4 * P].bitcast(BF16).rearrange("p (a c) -> p a c", c=P)
 
-        def aux_cp(m, kb, kh):
-            aps = aux_ps[m]
-            if m < QUADS:
-                qT[m] = qtp.tile([P, 4, P], BF16, name="qT", tag="qT")
-                nc.vector.tensor_copy(out=qT[m][:], in_=aps[:, 0:4, :])
-            if kb >= 1:
-                for g in range(2):
-                    k_copy("dve", kb, 2 * kh + g, aps[:, 4 + 2 * g : 6 + 2 * g, :])
-                if kh == 0:
-                    k_sinks(kb)
+        def aux_pe(m):
+            for n in range(4):
+                b, t = unit_of(2 * m + n // 2, n % 2)
+                u = NT * b + t
+                nc.tensor.transpose(q_ps[:, n, :], q_sb[u // 8][:, u % 8, :], ident[:])
+
+        def aux_cp(m):
+            qT[m] = qtp.tile([P, 4, P], BF16, name="qT", tag="qT")
+            nc.vector.tensor_copy(out=qT[m][:], in_=q_ps)
+
+        def k_pe(kb, kh):
+            for n in range(4):
+                nc.tensor.transpose(k_ps[:, n, :], k_sb[kb][:, 4 * kh + n, :], ident[:])
+
+        def k_cp(kb, kh):
+            for g in range(2):
+                k_copy("dve", kb, 2 * kh + g, k_ps[:, 2 * g : 2 * g + 2, :])
+            if kh == 0:
+                k_sinks(kb)
 
         k_first()
-        aux_pe(0, 0, 0)
-        aux_cp(0, 0, 0)
+        aux_pe(0)
+        aux_cp(0)
 
         s_ps, mx, nb, rs, rc, tps, grp, cod, scl, o_ps, o_sb = {}, {}, {}, {}, {}, {}, {}, {}, {}, {}, {}
 
         def ok(j):
             return 0 <= j < PAIRS
 
-        def st_qk(j):
-            for n in range(2):
+        def st_qk(j, n):
+            if True:
                 u = 2 * j + n
-                b, t = u // NT, u % NT
+                b, t = unit_of(j, n)
                 start, nsl, o, a, sink = plan(t)
                 s = ps_s.tile([P, 2, 16 * RUN], F32, name="s", tag="s")
                 s_ps[u] = s
@@ -259,7 +266,7 @@ def tile_swa_sinkmeta_t_kernel(tc, query_states, key_states, value_states, out):
             nb[j] = small.tile([P, 2], F32, name="nb", tag="nb")
             for n in range(2):
                 u = 2 * j + n
-                nsl = plan(u % NT)[1]
+                nsl = plan(unit_of(j, n)[1])[1]
                 nc.vector.tensor_reduce(out=mx[j][:, n : n + 1], in_=s_ps[u][:, :, 0 : 16 * nsl], axis=AX.XY, op=ALU.max)
             nc.scalar.activation(out=nb[j][:], in_=mx[j][:], func=ACTF.Copy, scale=-SCALE)
 
@@ -269,7 +276,7 @@ def tile_swa_sinkmeta_t_kernel(tc, query_states, key_states, value_states, out):
                 rs[m] = small.tile([P, 4], F32, name="rs", tag="rs")
             for n in range(2):
                 u = 2 * j + n
-                t = u % NT
+                t = unit_of(j, n)[1]
                 start, nsl, o, a, sink = plan(t)
                 nc.scalar.activation(
                     out=e_all[:, e_index(t), :, 16 * a : 16 * (a + nsl)],
@@ -281,7 +288,7 @@ def tile_swa_sinkmeta_t_kernel(tc, query_states, key_states, value_states, out):
         def st_tr(j):
             tps[j] = ps_t.tile([P, 2, 2, P], F32, name="tps", tag="tp")
             for n in range(2):
-                t = (2 * j + n) % NT
+                t = unit_of(j, n)[1]
                 words = e_all[:, e_index(t)].rearrange("p u c -> p (u c)").bitcast(F32)
                 for w in range(2):
                     nc.tensor.transpose(tps[j][:, n, w, :], words[:, P * w : P * (w + 1)], ident_f[:])
@@ -299,10 +306,9 @@ def tile_swa_sinkmeta_t_kernel(tc, query_states, key_states, value_states, out):
             )
 
         def st_mx(j):
-            o_ps[j] = ps_o.tile([P, 2, D], F32, name="o_ps", tag="o_ps")
+            o_ps[j] = oa[j % 2][:, 0 : 2 * D].rearrange("p (n d) -> p n d", d=D)
             for n in range(2):
-                u = 2 * j + n
-                b, t = u // NT, u % NT
+                b, t = unit_of(j, n)
                 o = plan(t)[2]
                 nc.tensor.matmul_mx(
                     out=o_ps[j][:, n, :],
@@ -322,13 +328,16 @@ def tile_swa_sinkmeta_t_kernel(tc, query_states, key_states, value_states, out):
             if h == 0:
                 o_sb[m] = osbp.tile([P, 4, D], F32, name="o_sb", tag="o_sb")
             nc.vector.tensor_tensor(
-                out=o_sb[m][:, 2 * h : 2 * h + 2, :], in0=o_ps[j][:],
+                out=o_sb[m][:, 2 * h : 2 * h + 2, :], in0=o_ps[j],
                 in1=rc[m][:, 2 * h : 2 * h + 2].unsqueeze(2).to_broadcast([P, 2, D]), op=ALU.mult,
             )
             if h == 1:
-                nc.sync.dma_start(out=o_view[:, 4 * m : 4 * m + 4, :], in_=o_sb[m][:])
+                b, t = unit_of(2 * m, 0)
+                nc.sync.dma_start(out=o_view[:, NT * b + t, :], in_=o_sb[m][:, 0, :])
+                b, t = unit_of(2 * m, 1)
+                nc.sync.dma_start(out=o_view[:, NT * b + t : NT * b + t + 3, :], in_=o_sb[m][:, 1:4, :])
 
-        FIRST_PAIR = (0, 7, 10, 13)
+        FIRST_PAIR = [min(x for x in range(NT) if plan(SEQ[x])[2] == o) // 2 for o in range(4)]
         v_regroup_at = {}
         v_quant_at = {}
         for b in range(B):
@@ -339,31 +348,29 @@ def tile_swa_sinkmeta_t_kernel(tc, query_states, key_states, value_states, out):
 
         for i in range(-2, PAIRS + 6):
             if ok(i + 1):
-                st_qk(i + 1)
-            kb, kh = 0, 0
-            if i % 2 == 0:
-                if i % 16 in (8, 10) and i // 16 + 1 < B:
-                    kb, kh = i // 16 + 1, (i % 16 - 8) // 2
-                if (i + 4) // 2 < QUADS or kb >= 1:
-                    aux_pe((i + 4) // 2, kb, kh)
+                st_qk(i + 1, 0)
+            if ok(i - 4):
+                st_mx(i - 4)
+            if ok(i + 1):
+                st_qk(i + 1, 1)
+            if i % 2 == 0 and (i + 4) // 2 < QUADS:
+                aux_pe((i + 4) // 2)
+            if i % 16 in (9, 11) and i // 16 + 1 < B:
+                k_pe(i // 16 + 1, (i % 16 - 9) // 2)
             if ok(i - 1):
                 st_tr(i - 1)
             if ok(i - 2):
                 st_regroup(i - 2)
-            if i % 2 == 1:
-                ip = i - 1
-                if ip % 16 in (8, 10) and ip // 16 + 1 < B:
-                    kb, kh = ip // 16 + 1, (ip % 16 - 8) // 2
-                if (ip + 4) // 2 < QUADS or kb >= 1:
-                    aux_cp((ip + 4) // 2, kb, kh)
+            if i % 2 == 1 and (i + 3) // 2 < QUADS:
+                aux_cp((i + 3) // 2)
+            if i % 16 in (10, 12) and i // 16 + 1 < B:
+                k_cp(i // 16 + 1, (i % 16 - 10) // 2)
             if ok(i):
                 st_exp(i)
             if ok(i - 3):
                 st_quant(i - 3)
             if ok(i - 5):
                 st_norm(i - 5)
-            if ok(i - 4):
-                st_mx(i - 4)
             if ok(i + 1):
                 st_max(i + 1)
             if i % 2 == 1 and ok(i - 2):

@@ -231,7 +231,7 @@ def tile_swa_sinkmeta_t_kernel(tc, query_states, key_states, value_states, out):
 
         def k_cp(kb, kh):
             for g in range(2):
-                k_copy("dve", kb, 2 * kh + g, k_ps[:, 2 * g : 2 * g + 2, :])
+                k_copy("act", kb, 2 * kh + g, k_ps[:, 2 * g : 2 * g + 2, :])
             if kh == 0:
                 k_sinks(kb)
 
@@ -268,12 +268,15 @@ def tile_swa_sinkmeta_t_kernel(tc, query_states, key_states, value_states, out):
                 u = 2 * j + n
                 nsl = plan(unit_of(j, n)[1])[1]
                 nc.vector.tensor_reduce(out=mx[j][:, n : n + 1], in_=s_ps[u][:, :, 0 : 16 * nsl], axis=AX.XY, op=ALU.max)
-            nc.scalar.activation(out=nb[j][:], in_=mx[j][:], func=ACTF.Copy, scale=-SCALE)
+                nc.gpsimd.tensor_scalar(
+                    out=nb[j][:, n : n + 1], in0=mx[j][:, n : n + 1],
+                    scalar1=-SCALE, scalar2=0.0, op0=ALU.mult, op1=ALU.add,
+                )
 
         def st_exp(j):
-            m, h = j // 2, j % 2
+            m, h = j // 4, j % 4
             if h == 0:
-                rs[m] = small.tile([P, 4], F32, name="rs", tag="rs")
+                rs[m] = small.tile([P, 8], F32, name="rs", tag="rs")
             for n in range(2):
                 u = 2 * j + n
                 t = unit_of(j, n)[1]
@@ -320,7 +323,7 @@ def tile_swa_sinkmeta_t_kernel(tc, query_states, key_states, value_states, out):
                 )
 
         def st_rc(m):
-            rc[m] = small.tile([P, 4], F32, name="rc", tag="rc")
+            rc[m] = small.tile([P, 8], F32, name="rc", tag="rc")
             nc.vector.reciprocal(out=rc[m][:], in_=rs[m][:])
 
         def st_norm(j):
@@ -329,7 +332,7 @@ def tile_swa_sinkmeta_t_kernel(tc, query_states, key_states, value_states, out):
                 o_sb[m] = osbp.tile([P, 4, D], F32, name="o_sb", tag="o_sb")
             nc.vector.tensor_tensor(
                 out=o_sb[m][:, 2 * h : 2 * h + 2, :], in0=o_ps[j],
-                in1=rc[m][:, 2 * h : 2 * h + 2].unsqueeze(2).to_broadcast([P, 2, D]), op=ALU.mult,
+                in1=rc[j // 4][:, 2 * (j % 4) : 2 * (j % 4) + 2].unsqueeze(2).to_broadcast([P, 2, D]), op=ALU.mult,
             )
             if h == 1:
                 b, t = unit_of(2 * m, 0)
@@ -373,8 +376,8 @@ def tile_swa_sinkmeta_t_kernel(tc, query_states, key_states, value_states, out):
                 st_norm(i - 5)
             if ok(i + 1):
                 st_max(i + 1)
-            if i % 2 == 1 and ok(i - 2):
-                st_rc((i - 2) // 2)
+            if i % 4 == 0 and ok(i - 1):
+                st_rc((i - 1) // 4)
             if i in v_quant_at:
                 quant_v(v_quant_at[i][0], v_quant_at[i][1])
             if i in v_regroup_at:

@@ -74,9 +74,9 @@ def tile_swa_sinkmeta_t_kernel(tc, query_states, key_states, value_states, out):
         codp = ctx.enter_context(tc.tile_pool(name="codp", bufs=3))
         osbp = ctx.enter_context(tc.tile_pool(name="osbp", bufs=6))
         small = ctx.enter_context(tc.tile_pool(name="small", bufs=8))
-        ps_s = ctx.enter_context(tc.psum_pool(name="ps_s", bufs=4))
+        ps_s = ctx.enter_context(tc.psum_pool(name="ps_s", bufs=5))
         ps_t = ctx.enter_context(tc.psum_pool(name="ps_t", bufs=2))
-        ps_oa = ctx.enter_context(tc.psum_pool(name="ps_oa", bufs=1))
+        ps_a = ctx.enter_context(tc.psum_pool(name="ps_a", bufs=1))
 
         q_view = query_states.rearrange("b s c -> (b s c)").rearrange(
             "(n r d) -> r n d", r=P, d=D
@@ -210,10 +210,9 @@ def tile_swa_sinkmeta_t_kernel(tc, query_states, key_states, value_states, out):
                     k_copy(eng, 0, 2 * half + g, kps[:, 2 * g : 2 * g + 2, :])
             k_sinks(0)
 
-        oa = [ps_oa.tile([P, 4 * P], F32, name="oa%d" % x) for x in range(2)]
-
-        q_ps = oa[0][:, 2 * P : 4 * P].bitcast(BF16).rearrange("p (a c) -> p a c", c=P)
-        k_ps = oa[1][:, 2 * P : 4 * P].bitcast(BF16).rearrange("p (a c) -> p a c", c=P)
+        aux = ps_a.tile([P, 8, P], BF16, name="aux")
+        q_ps = aux[:, 0:4, :]
+        k_ps = aux[:, 4:8, :]
 
         def aux_pe(m):
             for n in range(4):
@@ -244,14 +243,19 @@ def tile_swa_sinkmeta_t_kernel(tc, query_states, key_states, value_states, out):
         def ok(j):
             return 0 <= j < PAIRS
 
+        banks = {}
+
+        def st_bank(j, n):
+            banks[2 * j + n] = ps_s.tile([P, 4 * P], F32, name="s", tag="s")
+
         def st_qk(j, n):
             if True:
                 u = 2 * j + n
                 b, t = unit_of(j, n)
                 start, nsl, o, a, sink = plan(t)
-                s = ps_s.tile([P, 2, 16 * RUN], F32, name="s", tag="s")
+                s = banks[u][:, 0 : 32 * RUN].rearrange("p (u c) -> p u c", u=2)
                 s_ps[u] = s
-                slots = s[:].rearrange("p u (x c) -> p u x c", c=16)
+                slots = s.rearrange("p u (x c) -> p u x c", c=16)
                 ops = [(s[:, :, 0 : 16 * nsl], qT[j // 2][:, 2 * (j % 2) + n, :], kT[b][:, :, 16 * start : 16 * (start + nsl)])]
                 if t < 8:
                     ops.append((s[:, :, 16 * t : 16 * t + 16], ident[:], mask_b[:, K_LAST]))
@@ -261,10 +265,11 @@ def tile_swa_sinkmeta_t_kernel(tc, query_states, key_states, value_states, out):
                 for i, (o_ap, l_ap, r_ap) in enumerate(ops):
                     nc.tensor.matmul(out=o_ap, lhsT=l_ap, rhs=r_ap, start=(i == 0), stop=(i == len(ops) - 1))
 
-        def st_max(j):
-            mx[j] = small.tile([P, 2], F32, name="mx", tag="mx")
-            nb[j] = small.tile([P, 2], F32, name="nb", tag="nb")
-            for n in range(2):
+        def st_max(j, n):
+            if n == 0:
+                mx[j] = small.tile([P, 2], F32, name="mx", tag="mx")
+                nb[j] = small.tile([P, 2], F32, name="nb", tag="nb")
+            if True:
                 u = 2 * j + n
                 nsl = plan(unit_of(j, n)[1])[1]
                 nc.vector.tensor_reduce(out=mx[j][:, n : n + 1], in_=s_ps[u][:, :, 0 : 16 * nsl], axis=AX.XY, op=ALU.max)
@@ -274,9 +279,9 @@ def tile_swa_sinkmeta_t_kernel(tc, query_states, key_states, value_states, out):
                 )
 
         def st_exp(j):
-            m, h = j // 4, j % 4
+            m, h = j // 2, j % 2
             if h == 0:
-                rs[m] = small.tile([P, 8], F32, name="rs", tag="rs")
+                rs[m] = small.tile([P, 4], F32, name="rs", tag="rs")
             for n in range(2):
                 u = 2 * j + n
                 t = unit_of(j, n)[1]
@@ -308,33 +313,31 @@ def tile_swa_sinkmeta_t_kernel(tc, query_states, key_states, value_states, out):
                 in_=grp[j][:].rearrange("p n r w -> p (n r w)").bitcast(BF16),
             )
 
-        def st_mx(j):
-            o_ps[j] = oa[j % 2][:, 0 : 2 * D].rearrange("p (n d) -> p n d", d=D)
-            for n in range(2):
-                b, t = unit_of(j, n)
-                o = plan(t)[2]
-                nc.tensor.matmul_mx(
-                    out=o_ps[j][:, n, :],
-                    lhsT=cod[j][:, P * n : P * (n + 1)].bitcast(FP8X4),
-                    lhsT_scale=scl[j][:, P * n : P * (n + 1)],
-                    rhs=v_cod[o][:, D * b : D * (b + 1)].bitcast(FP8X4),
-                    rhs_scale=v_scl[o][:, D * b : D * (b + 1)],
-                    start=True, stop=True,
-                )
+        def st_mx(j, n):
+            b, t = unit_of(j, n)
+            o = plan(t)[2]
+            nc.tensor.matmul_mx(
+                out=banks[2 * (j + 5) + n][:, 32 * RUN : 32 * RUN + D],
+                lhsT=cod[j][:, P * n : P * (n + 1)].bitcast(FP8X4),
+                lhsT_scale=scl[j][:, P * n : P * (n + 1)],
+                rhs=v_cod[o][:, D * b : D * (b + 1)].bitcast(FP8X4),
+                rhs_scale=v_scl[o][:, D * b : D * (b + 1)],
+                start=True, stop=True,
+            )
 
         def st_rc(m):
-            rc[m] = small.tile([P, 8], F32, name="rc", tag="rc")
+            rc[m] = small.tile([P, 4], F32, name="rc", tag="rc")
             nc.vector.reciprocal(out=rc[m][:], in_=rs[m][:])
 
-        def st_norm(j):
+        def st_norm(j, n):
             m, h = j // 2, j % 2
-            if h == 0:
+            if h == 0 and n == 0:
                 o_sb[m] = osbp.tile([P, 4, D], F32, name="o_sb", tag="o_sb")
-            nc.vector.tensor_tensor(
-                out=o_sb[m][:, 2 * h : 2 * h + 2, :], in0=o_ps[j],
-                in1=rc[j // 4][:, 2 * (j % 4) : 2 * (j % 4) + 2].unsqueeze(2).to_broadcast([P, 2, D]), op=ALU.mult,
+            nc.vector.tensor_scalar(
+                out=o_sb[m][:, 2 * h + n, :], in0=banks[2 * (j + 5) + n][:, 32 * RUN : 32 * RUN + D],
+                scalar1=rc[m][:, 2 * h + n : 2 * h + n + 1], scalar2=None, op0=ALU.mult,
             )
-            if h == 1:
+            if h == 1 and n == 1:
                 b, t = unit_of(2 * m, 0)
                 nc.sync.dma_start(out=o_view[:, NT * b + t, :], in_=o_sb[m][:, 0, :])
                 b, t = unit_of(2 * m, 1)
@@ -349,35 +352,40 @@ def tile_swa_sinkmeta_t_kernel(tc, query_states, key_states, value_states, out):
                 v_quant_at[need - 2] = (o, b)
                 v_regroup_at[need - 5] = (o, b)
 
-        for i in range(-2, PAIRS + 6):
+        for i in range(-2, PAIRS + 5):
+            for n in range(2):
+                if ok(i + 1) or ok(i - 4):
+                    st_bank(i + 1, n)
             if ok(i + 1):
                 st_qk(i + 1, 0)
             if ok(i - 4):
-                st_mx(i - 4)
+                st_mx(i - 4, 0)
+                st_mx(i - 4, 1)
             if ok(i + 1):
                 st_qk(i + 1, 1)
             if i % 2 == 0 and (i + 4) // 2 < QUADS:
                 aux_pe((i + 4) // 2)
-            if i % 16 in (9, 11) and i // 16 + 1 < B:
-                k_pe(i // 16 + 1, (i % 16 - 9) // 2)
+            if i % 16 in (8, 10) and i // 16 + 1 < B:
+                k_pe(i // 16 + 1, (i % 16 - 8) // 2)
             if ok(i - 1):
                 st_tr(i - 1)
             if ok(i - 2):
                 st_regroup(i - 2)
             if i % 2 == 1 and (i + 3) // 2 < QUADS:
                 aux_cp((i + 3) // 2)
-            if i % 16 in (10, 12) and i // 16 + 1 < B:
-                k_cp(i // 16 + 1, (i % 16 - 10) // 2)
+            if i % 16 in (9, 11) and i // 16 + 1 < B:
+                k_cp(i // 16 + 1, (i % 16 - 9) // 2)
             if ok(i):
                 st_exp(i)
             if ok(i - 3):
                 st_quant(i - 3)
-            if ok(i - 5):
-                st_norm(i - 5)
-            if ok(i + 1):
-                st_max(i + 1)
-            if i % 4 == 0 and ok(i - 1):
-                st_rc((i - 1) // 4)
+            for n in range(2):
+                if ok(i + 1):
+                    st_max(i + 1, n)
+                if ok(i - 4):
+                    st_norm(i - 4, n)
+            if i % 2 == 0 and ok(i - 1):
+                st_rc((i - 1) // 2)
             if i in v_quant_at:
                 quant_v(v_quant_at[i][0], v_quant_at[i][1])
             if i in v_regroup_at:

@@ -91,11 +91,11 @@ def tile_swa_sinkmeta_t_kernel(tc, query_states, key_states, value_states, out):
         q_sb = [const.tile([P, 8, D], BF16, name="q_sb%d" % c) for c in range(UNITS // 8)]
         v_raw = [const.tile([P, B, 4 * D], BF16, name="v_raw%d" % o) for o in range(4)]
 
-        def load_k(b):
-            nc.sync.dma_start(out=k_sb[b][:], in_=k_view[:, 8 * b : 8 * b + 8, :])
+        def load_k(b, lo=0, hi=8):
+            nc.sync.dma_start(out=k_sb[b][:, lo:hi, :], in_=k_view[:, 8 * b + lo : 8 * b + hi, :])
 
-        def load_q(c):
-            nc.sync.dma_start(out=q_sb[c][:], in_=q_view[:, 8 * c : 8 * c + 8, :])
+        def load_q(c, lo=0, hi=8):
+            nc.sync.dma_start(out=q_sb[c][:, lo:hi, :], in_=q_view[:, 8 * c + lo : 8 * c + hi, :])
 
         def load_v(o):
             x = 0
@@ -108,9 +108,12 @@ def tile_swa_sinkmeta_t_kernel(tc, query_states, key_states, value_states, out):
                 )
                 x = y
 
-        load_k(0)
-        load_q(0)
-        load_q(1)
+        load_k(0, 0, 4)
+        load_q(0, 0, 1)
+        load_q(1, 0, 3)
+        load_k(0, 4, 8)
+        load_q(0, 1, 8)
+        load_q(1, 3, 8)
         load_v(0)
         load_q(2)
         load_v(1)
@@ -333,10 +336,16 @@ def tile_swa_sinkmeta_t_kernel(tc, query_states, key_states, value_states, out):
             m, h = j // 2, j % 2
             if h == 0 and n == 0:
                 o_sb[m] = osbp.tile([P, 4, D], F32, name="o_sb", tag="o_sb")
-            nc.vector.tensor_scalar(
-                out=o_sb[m][:, 2 * h + n, :], in0=banks[2 * (j + 5) + n][:, 32 * RUN : 32 * RUN + D],
-                scalar1=rc[m][:, 2 * h + n : 2 * h + n + 1], scalar2=None, op0=ALU.mult,
-            )
+            if (2 * j + n) % 8 == 0:
+                nc.scalar.activation(
+                    out=o_sb[m][:, 2 * h + n, :], in_=banks[2 * (j + 5) + n][:, 32 * RUN : 32 * RUN + D],
+                    func=ACTF.Copy, scale=rc[m][:, 2 * h + n : 2 * h + n + 1],
+                )
+            else:
+                nc.vector.tensor_scalar(
+                    out=o_sb[m][:, 2 * h + n, :], in0=banks[2 * (j + 5) + n][:, 32 * RUN : 32 * RUN + D],
+                    scalar1=rc[m][:, 2 * h + n : 2 * h + n + 1], scalar2=None, op0=ALU.mult,
+                )
             if h == 1 and n == 1:
                 b, t = unit_of(2 * m, 0)
                 nc.sync.dma_start(out=o_view[:, NT * b + t, :], in_=o_sb[m][:, 0, :])
@@ -350,7 +359,7 @@ def tile_swa_sinkmeta_t_kernel(tc, query_states, key_states, value_states, out):
             for o in range(4):
                 need = 16 * b + FIRST_PAIR[o] + 4
                 v_quant_at[need - 2] = (o, b)
-                v_regroup_at[need - 5] = (o, b)
+                v_regroup_at[need - 4] = (o, b)
 
         for i in range(-2, PAIRS + 5):
             for n in range(2):

@@ -74,6 +74,7 @@ def tile_swa_sinkmeta_t_kernel(tc, query_states, key_states, value_states, out):
         codp = ctx.enter_context(tc.tile_pool(name="codp", bufs=3))
         osbp = ctx.enter_context(tc.tile_pool(name="osbp", bufs=6))
         small = ctx.enter_context(tc.tile_pool(name="small", bufs=8))
+        scp = ctx.enter_context(tc.tile_pool(name="scp", bufs=6))
         ps_s = ctx.enter_context(tc.psum_pool(name="ps_s", bufs=5))
         ps_t = ctx.enter_context(tc.psum_pool(name="ps_t", bufs=2))
         ps_a = ctx.enter_context(tc.psum_pool(name="ps_a", bufs=1))
@@ -241,7 +242,7 @@ def tile_swa_sinkmeta_t_kernel(tc, query_states, key_states, value_states, out):
         aux_pe(0)
         aux_cp(0)
 
-        s_ps, mx, nb, rs, rc, tps, grp, cod, scl, o_ps, o_sb = {}, {}, {}, {}, {}, {}, {}, {}, {}, {}, {}
+        s_ps, s_sb, nb, rs, rc, tps, grp, cod, scl, o_ps, o_sb = {}, {}, {}, {}, {}, {}, {}, {}, {}, {}, {}
 
         def ok(j):
             return 0 <= j < PAIRS
@@ -270,15 +271,14 @@ def tile_swa_sinkmeta_t_kernel(tc, query_states, key_states, value_states, out):
 
         def st_max(j, n):
             if n == 0:
-                mx[j] = small.tile([P, 2], F32, name="mx", tag="mx")
                 nb[j] = small.tile([P, 2], F32, name="nb", tag="nb")
             if True:
                 u = 2 * j + n
                 nsl = plan(unit_of(j, n)[1])[1]
-                nc.vector.tensor_reduce(out=mx[j][:, n : n + 1], in_=s_ps[u][:, :, 0 : 16 * nsl], axis=AX.XY, op=ALU.max)
-                nc.gpsimd.tensor_scalar(
-                    out=nb[j][:, n : n + 1], in0=mx[j][:, n : n + 1],
-                    scalar1=-SCALE, scalar2=0.0, op0=ALU.mult, op1=ALU.add,
+                s_sb[u] = scp.tile([P, 2, 16 * RUN], F32, name="s_sb", tag="s_sb")
+                nc.vector.tensor_scalar(
+                    out=s_sb[u][:, :, 0 : 16 * nsl], in0=s_ps[u][:, :, 0 : 16 * nsl],
+                    scalar1=-SCALE, scalar2=None, op0=ALU.mult, op1=ALU.min, accum_out=nb[j][:, n : n + 1],
                 )
 
         def st_exp(j):
@@ -291,8 +291,8 @@ def tile_swa_sinkmeta_t_kernel(tc, query_states, key_states, value_states, out):
                 start, nsl, o, a, sink = plan(t)
                 nc.scalar.activation(
                     out=e_all[:, e_index(t), :, 16 * a : 16 * (a + nsl)],
-                    in_=s_ps[u][:, :, 0 : 16 * nsl],
-                    func=ACTF.Exp, bias=nb[j][:, n : n + 1], scale=SCALE,
+                    in_=s_sb[u][:, :, 0 : 16 * nsl],
+                    func=ACTF.Exp, bias=nb[j][:, n : n + 1], scale=-1.0,
                     accum_out=rs[m][:, 2 * h + n : 2 * h + n + 1],
                 )
 
@@ -336,7 +336,7 @@ def tile_swa_sinkmeta_t_kernel(tc, query_states, key_states, value_states, out):
             m, h = j // 2, j % 2
             if h == 0 and n == 0:
                 o_sb[m] = osbp.tile([P, 4, D], F32, name="o_sb", tag="o_sb")
-            if (2 * j + n) % 8 == 0:
+            if n == 0:
                 nc.scalar.activation(
                     out=o_sb[m][:, 2 * h + n, :], in_=banks[2 * (j + 5) + n][:, 32 * RUN : 32 * RUN + D],
                     func=ACTF.Copy, scale=rc[m][:, 2 * h + n : 2 * h + n + 1],
@@ -369,6 +369,7 @@ def tile_swa_sinkmeta_t_kernel(tc, query_states, key_states, value_states, out):
                 st_qk(i + 1, 0)
             if ok(i - 4):
                 st_mx(i - 4, 0)
+            if ok(i - 4):
                 st_mx(i - 4, 1)
             if ok(i + 1):
                 st_qk(i + 1, 1)
@@ -388,11 +389,14 @@ def tile_swa_sinkmeta_t_kernel(tc, query_states, key_states, value_states, out):
                 st_exp(i)
             if ok(i - 3):
                 st_quant(i - 3)
-            for n in range(2):
-                if ok(i + 1):
-                    st_max(i + 1, n)
-                if ok(i - 4):
-                    st_norm(i - 4, n)
+            if ok(i + 1):
+                st_max(i + 1, 0)
+            if ok(i - 4):
+                st_norm(i - 4, 0)
+            if ok(i + 1):
+                st_max(i + 1, 1)
+            if ok(i - 4):
+                st_norm(i - 4, 1)
             if i % 2 == 0 and ok(i - 1):
                 st_rc((i - 1) // 2)
             if i in v_quant_at:

@@ -33,6 +33,7 @@ SINK_SLOTS = (8, 17, 26)
 WINDOWS = (0, 7, 14, 19)
 K_FIRST, K_LAST, K_SINK, K_FIRST8, K_NONE = 0, 1, 2, 3, 4
 E_TILES = 15
+SCP = 8
 
 
 def eslot(block):
@@ -74,8 +75,9 @@ def tile_swa_sinkmeta_t_kernel(tc, query_states, key_states, value_states, out):
         codp = ctx.enter_context(tc.tile_pool(name="codp", bufs=3))
         osbp = ctx.enter_context(tc.tile_pool(name="osbp", bufs=6))
         small = ctx.enter_context(tc.tile_pool(name="small", bufs=8))
-        scp = ctx.enter_context(tc.tile_pool(name="scp", bufs=6))
-        ps_s = ctx.enter_context(tc.psum_pool(name="ps_s", bufs=5))
+        scp = ctx.enter_context(tc.tile_pool(name="scp", bufs=SCP))
+        ps_s = ctx.enter_context(tc.psum_pool(name="ps_s", bufs=3))
+        ps_m = ctx.enter_context(tc.psum_pool(name="ps_m", bufs=2))
         ps_t = ctx.enter_context(tc.psum_pool(name="ps_t", bufs=2))
         ps_a = ctx.enter_context(tc.psum_pool(name="ps_a", bufs=1))
 
@@ -226,7 +228,10 @@ def tile_swa_sinkmeta_t_kernel(tc, query_states, key_states, value_states, out):
 
         def aux_cp(m):
             qT[m] = qtp.tile([P, 4, P], BF16, name="qT", tag="qT")
-            nc.vector.tensor_copy(out=qT[m][:], in_=q_ps)
+            if True:
+                nc.scalar.copy(out=qT[m][:], in_=q_ps)
+            else:
+                nc.vector.tensor_copy(out=qT[m][:], in_=q_ps)
 
         def k_pe(kb, kh):
             for n in range(4):
@@ -249,12 +254,10 @@ def tile_swa_sinkmeta_t_kernel(tc, query_states, key_states, value_states, out):
 
         banks = {}
 
-        def st_bank(j, n):
-            banks[2 * j + n] = ps_s.tile([P, 4 * P], F32, name="s", tag="s")
-
         def st_qk(j, n):
             if True:
                 u = 2 * j + n
+                banks[u] = ps_s.tile([P, 4 * P], F32, name="s", tag="s")
                 b, t = unit_of(j, n)
                 start, nsl, o, a, sink = plan(t)
                 s = banks[u][:, 0 : 32 * RUN].rearrange("p (u c) -> p u c", u=2)
@@ -319,8 +322,11 @@ def tile_swa_sinkmeta_t_kernel(tc, query_states, key_states, value_states, out):
         def st_mx(j, n):
             b, t = unit_of(j, n)
             o = plan(t)[2]
+            m, h = j // 2, j % 2
+            if h == 0 and n == 0:
+                o_ps[m] = ps_m.tile([P, 4, D], F32, name="o_ps", tag="o_ps")
             nc.tensor.matmul_mx(
-                out=banks[2 * (j + 5) + n][:, 32 * RUN : 32 * RUN + D],
+                out=o_ps[m][:, 2 * h + n, :],
                 lhsT=cod[j][:, P * n : P * (n + 1)].bitcast(FP8X4),
                 lhsT_scale=scl[j][:, P * n : P * (n + 1)],
                 rhs=v_cod[o][:, D * b : D * (b + 1)].bitcast(FP8X4),
@@ -332,71 +338,62 @@ def tile_swa_sinkmeta_t_kernel(tc, query_states, key_states, value_states, out):
             rc[m] = small.tile([P, 4], F32, name="rc", tag="rc")
             nc.vector.reciprocal(out=rc[m][:], in_=rs[m][:])
 
-        def st_norm(j, n):
-            m, h = j // 2, j % 2
-            if h == 0 and n == 0:
-                o_sb[m] = osbp.tile([P, 4, D], F32, name="o_sb", tag="o_sb")
-            if n == 0:
-                nc.scalar.activation(
-                    out=o_sb[m][:, 2 * h + n, :], in_=banks[2 * (j + 5) + n][:, 32 * RUN : 32 * RUN + D],
-                    func=ACTF.Copy, scale=rc[m][:, 2 * h + n : 2 * h + n + 1],
-                )
+        def st_norm(m):
+            o_sb[m] = osbp.tile([P, 4, D], F32, name="o_sb", tag="o_sb")
+            if False:
+                for n in range(4):
+                    nc.scalar.activation(
+                        out=o_sb[m][:, n, :], in_=o_ps[m][:, n, :], func=ACTF.Copy, scale=rc[m][:, n : n + 1],
+                    )
             else:
-                nc.vector.tensor_scalar(
-                    out=o_sb[m][:, 2 * h + n, :], in0=banks[2 * (j + 5) + n][:, 32 * RUN : 32 * RUN + D],
-                    scalar1=rc[m][:, 2 * h + n : 2 * h + n + 1], scalar2=None, op0=ALU.mult,
+                nc.vector.tensor_tensor(
+                    out=o_sb[m][:], in0=o_ps[m][:], in1=rc[m][:].unsqueeze(2).to_broadcast([P, 4, D]), op=ALU.mult,
                 )
-            if h == 1 and n == 1:
-                b, t = unit_of(2 * m, 0)
-                nc.sync.dma_start(out=o_view[:, NT * b + t, :], in_=o_sb[m][:, 0, :])
-                b, t = unit_of(2 * m, 1)
-                nc.sync.dma_start(out=o_view[:, NT * b + t : NT * b + t + 3, :], in_=o_sb[m][:, 1:4, :])
+            b, t = unit_of(2 * m, 0)
+            nc.sync.dma_start(out=o_view[:, NT * b + t, :], in_=o_sb[m][:, 0, :])
+            b, t = unit_of(2 * m, 1)
+            nc.sync.dma_start(out=o_view[:, NT * b + t : NT * b + t + 3, :], in_=o_sb[m][:, 1:4, :])
 
         FIRST_PAIR = [min(x for x in range(NT) if plan(SEQ[x])[2] == o) // 2 for o in range(4)]
         v_regroup_at = {}
         v_quant_at = {}
         for b in range(B):
             for o in range(4):
-                need = 16 * b + FIRST_PAIR[o] + 4
+                need = 16 * b + FIRST_PAIR[o] + 5
                 v_quant_at[need - 2] = (o, b)
                 v_regroup_at[need - 4] = (o, b)
 
-        for i in range(-2, PAIRS + 5):
-            for n in range(2):
-                if ok(i + 1) or ok(i - 4):
-                    st_bank(i + 1, n)
-            if ok(i + 1):
-                st_qk(i + 1, 0)
-            if ok(i - 4):
-                st_mx(i - 4, 0)
-            if ok(i - 4):
-                st_mx(i - 4, 1)
-            if ok(i + 1):
-                st_qk(i + 1, 1)
-            if i % 2 == 0 and (i + 4) // 2 < QUADS:
-                aux_pe((i + 4) // 2)
-            if i % 16 in (8, 10) and i // 16 + 1 < B:
+        for i in range(-3, PAIRS + 7):
+            if ok(i + 2):
+                st_qk(i + 2, 0)
+            if ok(i - 5):
+                st_mx(i - 5, 0)
+            if ok(i - 5):
+                st_mx(i - 5, 1)
+            if ok(i + 2):
+                st_qk(i + 2, 1)
+            if (i + 2) % 2 == 1 and 0 < (i + 2 + 3) // 2 < QUADS:
+                aux_pe((i + 2 + 3) // 2)
+            if i % 16 in (8, 10) and i // 16 + 1 < B and i > 0:
                 k_pe(i // 16 + 1, (i % 16 - 8) // 2)
             if ok(i - 1):
                 st_tr(i - 1)
             if ok(i - 2):
                 st_regroup(i - 2)
-            if i % 2 == 1 and (i + 3) // 2 < QUADS:
-                aux_cp((i + 3) // 2)
-            if i % 16 in (9, 11) and i // 16 + 1 < B:
+            if (i + 2) % 2 == 0 and 0 < (i + 2 + 2) // 2 < QUADS:
+                aux_cp((i + 2 + 2) // 2)
+            if i % 16 in (9, 11) and i // 16 + 1 < B and i > 0:
                 k_cp(i // 16 + 1, (i % 16 - 9) // 2)
             if ok(i):
                 st_exp(i)
-            if ok(i - 3):
-                st_quant(i - 3)
-            if ok(i + 1):
-                st_max(i + 1, 0)
             if ok(i - 4):
-                st_norm(i - 4, 0)
-            if ok(i + 1):
-                st_max(i + 1, 1)
-            if ok(i - 4):
-                st_norm(i - 4, 1)
+                st_quant(i - 4)
+            if ok(i + 2):
+                st_max(i + 2, 0)
+            if ok(i + 2):
+                st_max(i + 2, 1)
+            if (i - 6) % 2 == 1 and ok(i - 6):
+                st_norm((i - 6) // 2)
             if i % 2 == 0 and ok(i - 1):
                 st_rc((i - 1) // 2)
             if i in v_quant_at:

@@ -20,7 +20,6 @@ BLK = 32
 POS = P // H
 NT = S // POS
 UNITS = B * NT
-PAIRS = UNITS // 2
 QUADS = UNITS // 4
 RUN = 10
 SCALE = 1.0 / math.sqrt(D)
@@ -30,10 +29,10 @@ FLOPS = 4 * D * ALLOWED * B * H
 
 E_SLOTS = 35
 SINK_SLOTS = (8, 17, 26)
-WINDOWS = (0, 7, 14, 19)
 K_FIRST, K_LAST, K_SINK, K_FIRST8, K_NONE = 0, 1, 2, 3, 4
-E_TILES = 15
-SCP = 8
+WINDOWS = (0, 16, 3, 19)
+LEAD = 4
+LAG = 14
 
 
 def eslot(block):
@@ -46,23 +45,64 @@ def eblock(slot):
 
 def plan(t):
     if t < 8:
-        start, n, sink = 0, t + 1, None
-    else:
-        start, n = eslot(t - 8), RUN
-        sink = [x for x in SINK_SLOTS if start < x < start + n][0] - start
-    o = min(start // 7, 3)
-    return start, n, o, start - WINDOWS[o], sink
+        return 0, t + 1, None
+    start = eslot(t - 8)
+    return start, RUN, [x for x in SINK_SLOTS if start < x < start + RUN][0] - start
 
 
-def e_index(t):
-    return plan(t)[3] if t >= 8 else 7 + t
+PACKS = [
+    ((2, 3), (0, 0)), ((4,), (0,)),
+    ((5, 14, 23), (0, 1)), ((6, 15, 24), (0, 1)), ((7, 16, 25), (0, 1)), ((8, 17, 26), (0, 1)),
+    ((0, 9, 18, 27), (0, 1)), ((1, 10, 19, 28), (0, 1)),
+    ((11, 20, 29), (2, 3)), ((12, 21, 30), (2, 3)), ((13, 22, 31), (2, 3)),
+]
+NG = len(PACKS)
 
 
-SEQ = [t for lead in range(8) for t in (lead, 8 + 3 * lead, 9 + 3 * lead, 10 + 3 * lead)]
+def place(g, k):
+    units, opers = PACKS[g]
+    start, n = plan(units[k])[0:2]
+    a = 16 * k if opers[-1] == 0 else start - WINDOWS[opers[0]]
+    parts = [
+        (p, max(a, 16 * p) - 16 * p, min(a + n, 16 * p + 16) - 16 * p)
+        for p in range(len(opers))
+        if a < 16 * p + 16 and a + n > 16 * p
+    ]
+    return a, parts
 
 
-def unit_of(j, n):
-    return (2 * j + n) // NT, SEQ[(2 * j + n) % NT]
+def crowd(g, p):
+    return len([1 for k in range(len(PACKS[g][0])) for part in place(g, k)[1] if part[0] == p])
+
+
+def behind(g, p):
+    return max([part[2] for k in range(len(PACKS[g][0])) for part in place(g, k)[1] if part[0] == p])
+
+
+def scale_row(y):
+    return 32 * (y // 4) + y % 4
+
+
+MASKED = sorted(
+    [
+        (hi == behind(g, p), PACKS[g][1][p], g, k, p, lo, hi)
+        for g in range(NG)
+        for k in range(len(PACKS[g][0]))
+        for p, lo, hi in place(g, k)[1]
+        if crowd(g, p) > 1
+    ]
+)
+MASKED = [mask[2:7] for mask in MASKED]
+NM = len(MASKED)
+NZ = len([1 for g, k, p, lo, hi in MASKED if hi < behind(g, p)])
+MASK_OF = {MASKED[j][0:3]: j for j in range(NM)}
+NTB = 2
+QP, KP = 7, 17
+LQ = [6, 34, 66]
+ND = 2
+SEQ = [(b, PACKS[g][0][k], g, k) for b in range(B) for g in range(NG) for k in range(len(PACKS[g][0]))]
+GROUPS = [(x, len(PACKS[SEQ[x][2]][0]), SEQ[x][0], SEQ[x][2]) for x in range(UNITS) if SEQ[x][3] == 0]
+GROUP_OF = [len([1 for grp in GROUPS if grp[0] <= x]) - 1 for x in range(UNITS)]
 
 
 def tile_swa_sinkmeta_t_kernel(tc, query_states, key_states, value_states, out):
@@ -72,10 +112,10 @@ def tile_swa_sinkmeta_t_kernel(tc, query_states, key_states, value_states, out):
         const = ctx.enter_context(tc.tile_pool(name="const", bufs=1))
         qtp = ctx.enter_context(tc.tile_pool(name="qtp", bufs=4))
         grpp = ctx.enter_context(tc.tile_pool(name="grpp", bufs=3))
-        codp = ctx.enter_context(tc.tile_pool(name="codp", bufs=3))
-        osbp = ctx.enter_context(tc.tile_pool(name="osbp", bufs=6))
+        codp = ctx.enter_context(tc.tile_pool(name="codp", bufs=4))
+        osbp = ctx.enter_context(tc.tile_pool(name="osbp", bufs=8))
         small = ctx.enter_context(tc.tile_pool(name="small", bufs=8))
-        scp = ctx.enter_context(tc.tile_pool(name="scp", bufs=SCP))
+        scp = ctx.enter_context(tc.tile_pool(name="scp", bufs=8))
         ps_s = ctx.enter_context(tc.psum_pool(name="ps_s", bufs=3))
         ps_m = ctx.enter_context(tc.psum_pool(name="ps_m", bufs=2))
         ps_t = ctx.enter_context(tc.psum_pool(name="ps_t", bufs=2))
@@ -87,18 +127,15 @@ def tile_swa_sinkmeta_t_kernel(tc, query_states, key_states, value_states, out):
         o_view = out.rearrange("b s c -> (b s c)").rearrange("(n r d) -> r n d", r=P, d=D)
         k_view = key_states.rearrange("b (a p) d -> p (b a) d", p=P)
 
-        def v_rows(k0, nkeys):
-            return value_states[:, k0 : k0 + nkeys, :].rearrange("b (p t) d -> p b (t d)", t=4)
-
         k_sb = [const.tile([P, 8, D], BF16, name="k_sb%d" % b) for b in range(B)]
-        q_sb = [const.tile([P, 8, D], BF16, name="q_sb%d" % c) for c in range(UNITS // 8)]
+        q_sb = [const.tile([P, NT, D], BF16, name="q_sb%d" % b) for b in range(B)]
         v_raw = [const.tile([P, B, 4 * D], BF16, name="v_raw%d" % o) for o in range(4)]
 
         def load_k(b, lo=0, hi=8):
             nc.sync.dma_start(out=k_sb[b][:, lo:hi, :], in_=k_view[:, 8 * b + lo : 8 * b + hi, :])
 
-        def load_q(c, lo=0, hi=8):
-            nc.sync.dma_start(out=q_sb[c][:, lo:hi, :], in_=q_view[:, 8 * c + lo : 8 * c + hi, :])
+        def load_q(b, lo=0, hi=NT):
+            nc.sync.dma_start(out=q_sb[b][:, lo:hi, :], in_=q_view[:, NT * b + lo : NT * b + hi, :])
 
         def load_v(o):
             x = 0
@@ -106,32 +143,34 @@ def tile_swa_sinkmeta_t_kernel(tc, query_states, key_states, value_states, out):
                 y = x + 1
                 while y < 16 and eblock(WINDOWS[o] + y) == eblock(WINDOWS[o] + y - 1) + 1:
                     y += 1
+                k0, nkeys = BLK * eblock(WINDOWS[o] + x), BLK * (y - x)
                 nc.sync.dma_start(
-                    out=v_raw[o][8 * x : 8 * y], in_=v_rows(BLK * eblock(WINDOWS[o] + x), BLK * (y - x))
+                    out=v_raw[o][8 * x : 8 * y],
+                    in_=value_states[:, k0 : k0 + nkeys, :].rearrange("b (p t) d -> p b (t d)", t=4),
                 )
                 x = y
 
         load_k(0, 0, 4)
-        load_q(0, 0, 1)
-        load_q(1, 0, 3)
+        load_q(0, 2, 6)
+        load_q(0, 14, 17)
+        load_q(0, 23, 26)
+        load_q(0, 6, 9)
         load_k(0, 4, 8)
-        load_q(0, 1, 8)
-        load_q(1, 3, 8)
+        load_q(0, 17, 20)
+        load_q(0, 26, 29)
+        load_q(0, 0, 2)
         load_v(0)
-        load_q(2)
+        load_q(0, 9, 14)
         load_v(1)
-        load_q(3)
+        load_q(0, 20, 23)
+        load_q(0, 29, 32)
         load_v(2)
         load_v(3)
         for b in range(1, B):
             load_k(b)
-            for c in range(4 * b, 4 * b + 4):
-                load_q(c)
 
         ident = const.tile([P, P], BF16, name="ident")
         make_identity(nc, ident[:])
-        ident_f = const.tile([P, P], F32, name="ident_f")
-        make_identity(nc, ident_f[:])
         mask_f = const.tile([P, 2, BLK], F32, name="mask_f")
         nc.gpsimd.memset(mask_f[:], 0.0)
         nc.gpsimd.affine_select(
@@ -147,12 +186,9 @@ def tile_swa_sinkmeta_t_kernel(tc, query_states, key_states, value_states, out):
         nc.vector.memset(warm[:], 0.0)
         nc.scalar.activation(out=warm[:], in_=warm[:], func=ACTF.Exp)
 
-        e_all = const.tile([P, E_TILES, 2, 2 * P], BF16, name="e_all")
+        v_msk = const.tile([P, NM, B * D], U8, name="v_msk", align_bytes=64)
+        nc.vector.memset(v_msk[:, 0:NZ].rearrange("p m d -> p (m d)").bitcast(I32), 0)
 
-        def zero_e(lo, hi):
-            nc.vector.memset(e_all[:, lo:hi].rearrange("p k u c -> p (k u c)").bitcast(I32), 0)
-
-        zero_e(7, 12)
         mask_b = const.tile([P, 5, 2, 16], BF16, name="mask_b")
         for kind in (K_FIRST, K_LAST):
             nc.vector.tensor_copy(
@@ -168,8 +204,30 @@ def tile_swa_sinkmeta_t_kernel(tc, query_states, key_states, value_states, out):
         for w, kind in ((0, K_FIRST), (1, K_FIRST8)):
             nc.vector.tensor_copy(out=mask_fl[:, w, :, 0, :], in_=mask_b[:, kind])
             nc.vector.tensor_copy(out=mask_fl[:, w, :, 1, :], in_=mask_b[:, K_LAST])
-        zero_e(12, E_TILES)
-        zero_e(0, 7)
+
+        e_all = [const.tile([P, 2, 256 * len(PACKS[g][1])], BF16, name="e_all%d" % g) for g in range(NG)]
+
+        def zero_e(g):
+            taken = []
+            for k in range(len(PACKS[g][0])):
+                a = place(g, k)[0]
+                taken += [x for x in range(a, a + plan(PACKS[g][0][k])[1])]
+            n = 16 * len(PACKS[g][1])
+            x = 0
+            while x < n:
+                y = x
+                while y < n and y not in taken:
+                    y += 1
+                if y > x:
+                    nc.gpsimd.memset(e_all[g][:, :, 16 * x : 16 * y].bitcast(I32), 0)
+                x = y + 1
+
+        zero_e(0)
+        zero_e(1)
+        ident_f = const.tile([P, P], F32, name="ident_f")
+        make_identity(nc, ident_f[:])
+        for g in range(2, NG):
+            zero_e(g)
 
         v_grp = [const.tile([P, B, D, 4], BF16, name="v_grp%d" % o, align_bytes=64) for o in range(4)]
         v_cod = [const.tile([P, B * D], U32, name="v_cod%d" % o, align_bytes=64) for o in range(4)]
@@ -189,16 +247,30 @@ def tile_swa_sinkmeta_t_kernel(tc, query_states, key_states, value_states, out):
                 in_=v_grp[o][:, b].rearrange("p d t -> p (d t)"),
             )
 
+        def mask_v(j0, j1, b0, b1):
+            g, k, p, lo, hi = MASKED[j0]
+            o = PACKS[g][1][p]
+            cols = slice(D * b0, D * b1)
+            rows = slice(0, scale_row(hi - 1) + 1 if j0 < NZ else P)
+            src = v_scl[o][rows, cols].bitcast(I32)
+            nc.gpsimd.tensor_copy(
+                out=v_msk[rows, j0:j1, cols].bitcast(I32),
+                in_=src.unsqueeze(1).to_broadcast([rows.stop, j1 - j0, (b1 - b0) * D // 4]),
+            )
+
+        def clear_v(j, b0, b1):
+            lo = MASKED[j][3]
+            if lo > 0:
+                nc.gpsimd.memset(v_msk[0 : scale_row(lo - 1) + 1, j, D * b0 : D * b1].bitcast(I32), 0)
+
         kT = [const.tile([P, 2, 16 * (E_SLOTS + 1)], BF16, name="kT%d" % b) for b in range(B)]
         qT = {}
 
-        def k_copy(eng, b, grp8, src):
-            dst = kT[b][:, :, 144 * grp8 : 144 * grp8 + 128].rearrange("p u (g e) -> p u g e", e=2)
-            view = src.rearrange("p a c -> p (a c)").rearrange("p (g u e) -> p u g e", u=2, e=2)
-            if eng == "act":
-                nc.scalar.copy(out=dst, in_=view)
-            else:
-                nc.vector.tensor_copy(out=dst, in_=view)
+        def k_copy(b, grp8, src):
+            nc.scalar.copy(
+                out=kT[b][:, :, 144 * grp8 : 144 * grp8 + 128].rearrange("p u (g e) -> p u g e", e=2),
+                in_=src.rearrange("p a c -> p (a c)").rearrange("p (g u e) -> p u g e", u=2, e=2),
+            )
 
         def k_sinks(b):
             nc.gpsimd.tensor_scalar(
@@ -207,26 +279,25 @@ def tile_swa_sinkmeta_t_kernel(tc, query_states, key_states, value_states, out):
                 scalar1=1.0, scalar2=0.0, op0=ALU.mult, op1=ALU.add,
             )
 
-        def k_first():
-            for half, eng in ((0, "act"), (1, "dve")):
-                kps = ps_t.tile([P, 4, P], BF16, name="kps", tag="tp")
-                for a in range(4):
-                    nc.tensor.transpose(kps[:, a, :], k_sb[0][:, 4 * half + a, :], ident[:])
-                for g in range(2):
-                    k_copy(eng, 0, 2 * half + g, kps[:, 2 * g : 2 * g + 2, :])
-            k_sinks(0)
+        def k_first(half):
+            kps = ps_t.tile([P, 4, P], BF16, name="kps", tag="tp")
+            for a in range(4):
+                nc.tensor.transpose(kps[:, a, :], k_sb[0][:, 4 * half + a, :], ident[:])
+            for g in range(2):
+                k_copy(0, 2 * half + g, kps[:, 2 * g : 2 * g + 2, :])
+            if half == 0:
+                k_sinks(0)
 
         aux = ps_a.tile([P, 8, P], BF16, name="aux")
         q_ps = aux[:, 0:4, :]
         k_ps = aux[:, 4:8, :]
 
-        def aux_pe(m):
+        def q_pe(m):
             for n in range(4):
-                b, t = unit_of(2 * m + n // 2, n % 2)
-                u = NT * b + t
-                nc.tensor.transpose(q_ps[:, n, :], q_sb[u // 8][:, u % 8, :], ident[:])
+                b, t = SEQ[4 * m + n][0:2]
+                nc.tensor.transpose(q_ps[:, n, :], q_sb[b][:, t, :], ident[:])
 
-        def aux_cp(m):
+        def q_cp(m):
             qT[m] = qtp.tile([P, 4, P], BF16, name="qT", tag="qT")
             if True:
                 nc.scalar.copy(out=qT[m][:], in_=q_ps)
@@ -239,164 +310,211 @@ def tile_swa_sinkmeta_t_kernel(tc, query_states, key_states, value_states, out):
 
         def k_cp(kb, kh):
             for g in range(2):
-                k_copy("act", kb, 2 * kh + g, k_ps[:, 2 * g : 2 * g + 2, :])
+                k_copy(kb, 2 * kh + g, k_ps[:, 2 * g : 2 * g + 2, :])
             if kh == 0:
                 k_sinks(kb)
 
-        k_first()
-        aux_pe(0)
-        aux_cp(0)
+        k_first(0)
+        q_pe(0)
+        q_cp(0)
 
         s_ps, s_sb, nb, rs, rc, tps, grp, cod, scl, o_ps, o_sb = {}, {}, {}, {}, {}, {}, {}, {}, {}, {}, {}
 
-        def ok(j):
-            return 0 <= j < PAIRS
+        def st_qk(x):
+            b, t = SEQ[x][0:2]
+            start, nsl, sink = plan(t)
+            bank = ps_s.tile([P, 4 * P], F32, name="s", tag="s")
+            s = bank[:, 0 : 32 * RUN].rearrange("p (u c) -> p u c", u=2)
+            s_ps[x] = s
+            slots = s.rearrange("p u (x c) -> p u x c", c=16)
+            ops = [(s[:, :, 0 : 16 * nsl], qT[x // 4][:, x % 4, :], kT[b][:, :, 16 * start : 16 * (start + nsl)])]
+            if t < 8:
+                ops.append((s[:, :, 16 * t : 16 * t + 16], ident[:], mask_b[:, K_LAST]))
+            else:
+                ops.append((slots[:, :, 0:RUN:RUN - 1, :], ident[:], mask_fl[:, 1 if t == 8 else 0]))
+                ops.append((s[:, :, 16 * sink : 16 * sink + 16], ident[:], mask_b[:, K_NONE if t == 8 else K_SINK]))
+            for i, (o_ap, l_ap, r_ap) in enumerate(ops):
+                nc.tensor.matmul(out=o_ap, lhsT=l_ap, rhs=r_ap, start=(i == 0), stop=(i == len(ops) - 1))
 
-        banks = {}
-
-        def st_qk(j, n):
-            if True:
-                u = 2 * j + n
-                banks[u] = ps_s.tile([P, 4 * P], F32, name="s", tag="s")
-                b, t = unit_of(j, n)
-                start, nsl, o, a, sink = plan(t)
-                s = banks[u][:, 0 : 32 * RUN].rearrange("p (u c) -> p u c", u=2)
-                s_ps[u] = s
-                slots = s.rearrange("p u (x c) -> p u x c", c=16)
-                ops = [(s[:, :, 0 : 16 * nsl], qT[j // 2][:, 2 * (j % 2) + n, :], kT[b][:, :, 16 * start : 16 * (start + nsl)])]
-                if t < 8:
-                    ops.append((s[:, :, 16 * t : 16 * t + 16], ident[:], mask_b[:, K_LAST]))
-                else:
-                    ops.append((slots[:, :, 0:RUN:RUN - 1, :], ident[:], mask_fl[:, 1 if t == 8 else 0]))
-                    ops.append((s[:, :, 16 * sink : 16 * sink + 16], ident[:], mask_b[:, K_NONE if t == 8 else K_SINK]))
-                for i, (o_ap, l_ap, r_ap) in enumerate(ops):
-                    nc.tensor.matmul(out=o_ap, lhsT=l_ap, rhs=r_ap, start=(i == 0), stop=(i == len(ops) - 1))
-
-        def st_max(j, n):
+        def st_max(x):
+            j, n = x // 2, x % 2
             if n == 0:
                 nb[j] = small.tile([P, 2], F32, name="nb", tag="nb")
-            if True:
-                u = 2 * j + n
-                nsl = plan(unit_of(j, n)[1])[1]
-                s_sb[u] = scp.tile([P, 2, 16 * RUN], F32, name="s_sb", tag="s_sb")
-                nc.vector.tensor_scalar(
-                    out=s_sb[u][:, :, 0 : 16 * nsl], in0=s_ps[u][:, :, 0 : 16 * nsl],
-                    scalar1=-SCALE, scalar2=None, op0=ALU.mult, op1=ALU.min, accum_out=nb[j][:, n : n + 1],
-                )
+            nsl = plan(SEQ[x][1])[1]
+            s_sb[x] = scp.tile([P, 2, 16 * RUN], F32, name="s_sb", tag="s_sb")
+            nc.vector.tensor_scalar(
+                out=s_sb[x][:, :, 0 : 16 * nsl], in0=s_ps[x][:, :, 0 : 16 * nsl],
+                scalar1=-SCALE, scalar2=None, op0=ALU.mult, op1=ALU.min, accum_out=nb[j][:, n : n + 1],
+            )
 
-        def st_exp(j):
-            m, h = j // 2, j % 2
-            if h == 0:
-                rs[m] = small.tile([P, 4], F32, name="rs", tag="rs")
-            for n in range(2):
-                u = 2 * j + n
-                t = unit_of(j, n)[1]
-                start, nsl, o, a, sink = plan(t)
-                nc.scalar.activation(
-                    out=e_all[:, e_index(t), :, 16 * a : 16 * (a + nsl)],
-                    in_=s_sb[u][:, :, 0 : 16 * nsl],
-                    func=ACTF.Exp, bias=nb[j][:, n : n + 1], scale=-1.0,
-                    accum_out=rs[m][:, 2 * h + n : 2 * h + n + 1],
-                )
+        def st_exp(x):
+            m, n = x // 8, x % 8
+            if n == 0:
+                rs[m] = small.tile([P, 8], F32, name="rs", tag="rs")
+            b, t, g, k = SEQ[x]
+            nsl = plan(t)[1]
+            a = place(g, k)[0]
+            nc.scalar.activation(
+                out=e_all[g][:, :, 16 * a : 16 * (a + nsl)],
+                in_=s_sb[x][:, :, 0 : 16 * nsl],
+                func=ACTF.Exp, bias=nb[x // 2][:, x % 2 : x % 2 + 1], scale=-1.0,
+                accum_out=rs[m][:, n : n + 1],
+            )
 
-        def st_tr(j):
-            tps[j] = ps_t.tile([P, 2, 2, P], F32, name="tps", tag="tp")
-            for n in range(2):
-                t = unit_of(j, n)[1]
-                words = e_all[:, e_index(t)].rearrange("p u c -> p (u c)").bitcast(F32)
-                for w in range(2):
-                    nc.tensor.transpose(tps[j][:, n, w, :], words[:, P * w : P * (w + 1)], ident_f[:])
+        def st_tr(i):
+            g = GROUPS[i][3]
+            np_ = len(PACKS[g][1])
+            tps[i] = ps_t.tile([P, np_, 2, P], F32, name="tps", tag="tp")
+            for p in range(np_):
+                for u in range(2):
+                    words = e_all[g][:, u, 256 * p : 256 * (p + 1)].bitcast(F32)
+                    nc.tensor.transpose(tps[i][:, p, u, :], words, ident_f[:])
 
-        def st_regroup(j):
-            grp[j] = grpp.tile([P, 2, P, 2], F32, name="grp", tag="grp", align_bytes=64)
-            nc.scalar.copy(out=grp[j][:], in_=tps[j][:].rearrange("p n w r -> p n r w"))
+        def st_regroup(i):
+            np_ = len(PACKS[GROUPS[i][3]][1])
+            grp[i] = grpp.tile([P, np_, P, 2], F32, name="grp", tag="grp", align_bytes=64)
+            nc.scalar.copy(out=grp[i][:], in_=tps[i][:].rearrange("p n w r -> p n r w"))
 
-        def st_quant(j):
-            cod[j] = codp.tile([P, 2 * P], U32, name="cod", tag="cod", align_bytes=64)
-            scl[j] = codp.tile([P, 2 * P], U8, name="scl", tag="scl", align_bytes=64)
+        def st_quant(i):
+            np_ = len(PACKS[GROUPS[i][3]][1])
+            cod[i] = codp.tile([P, np_ * P], U32, name="cod", tag="cod", align_bytes=64)
+            scl[i] = codp.tile([P, np_ * P], U8, name="scl", tag="scl", align_bytes=64)
             nc.vector.quantize_mx(
-                out=cod[j][:].bitcast(FP8X4), scales=scl[j][:],
-                in_=grp[j][:].rearrange("p n r w -> p (n r w)").bitcast(BF16),
+                out=cod[i][:].bitcast(FP8X4), scales=scl[i][:],
+                in_=grp[i][:].rearrange("p n r w -> p (n r w)").bitcast(BF16),
             )
 
-        def st_mx(j, n):
-            b, t = unit_of(j, n)
-            o = plan(t)[2]
-            m, h = j // 2, j % 2
-            if h == 0 and n == 0:
-                o_ps[m] = ps_m.tile([P, 4, D], F32, name="o_ps", tag="o_ps")
-            nc.tensor.matmul_mx(
-                out=o_ps[m][:, 2 * h + n, :],
-                lhsT=cod[j][:, P * n : P * (n + 1)].bitcast(FP8X4),
-                lhsT_scale=scl[j][:, P * n : P * (n + 1)],
-                rhs=v_cod[o][:, D * b : D * (b + 1)].bitcast(FP8X4),
-                rhs_scale=v_scl[o][:, D * b : D * (b + 1)],
-                start=True, stop=True,
-            )
+        def st_mx(x):
+            i = GROUP_OF[x]
+            b, t, g, k = SEQ[x]
+            if x % 4 == 0:
+                o_ps[x // 4] = ps_m.tile([P, 4, D], F32, name="o_ps", tag="o_ps")
+            parts = place(g, k)[1]
+            for y in range(len(parts)):
+                p = parts[y][0]
+                o = PACKS[g][1][p]
+                masked = (g, k, p) in MASK_OF
+                cols = slice(D * b, D * (b + 1))
+                scales = v_msk[:, MASK_OF[g, k, p], cols] if masked else v_scl[o][:, cols]
+                nc.tensor.matmul_mx(
+                    out=o_ps[x // 4][:, x % 4, :],
+                    lhsT=cod[i][:, P * p : P * (p + 1)].bitcast(FP8X4),
+                    lhsT_scale=scl[i][:, P * p : P * (p + 1)],
+                    rhs=v_cod[o][:, cols].bitcast(FP8X4),
+                    rhs_scale=scales,
+                    start=(y == 0), stop=(y == len(parts) - 1),
+                )
 
         def st_rc(m):
-            rc[m] = small.tile([P, 4], F32, name="rc", tag="rc")
+            rc[m] = small.tile([P, 8], F32, name="rc", tag="rc")
             nc.vector.reciprocal(out=rc[m][:], in_=rs[m][:])
 
         def st_norm(m):
             o_sb[m] = osbp.tile([P, 4, D], F32, name="o_sb", tag="o_sb")
+            scales = rc[m // 2][:, 4 * (m % 2) : 4 * (m % 2) + 4]
             if False:
                 for n in range(4):
                     nc.scalar.activation(
-                        out=o_sb[m][:, n, :], in_=o_ps[m][:, n, :], func=ACTF.Copy, scale=rc[m][:, n : n + 1],
+                        out=o_sb[m][:, n, :], in_=o_ps[m][:, n, :], func=ACTF.Copy, scale=scales[:, n : n + 1],
                     )
             else:
                 nc.vector.tensor_tensor(
-                    out=o_sb[m][:], in0=o_ps[m][:], in1=rc[m][:].unsqueeze(2).to_broadcast([P, 4, D]), op=ALU.mult,
+                    out=o_sb[m][:], in0=o_ps[m][:], in1=scales.unsqueeze(2).to_broadcast([P, 4, D]), op=ALU.mult,
                 )
-            b, t = unit_of(2 * m, 0)
-            nc.sync.dma_start(out=o_view[:, NT * b + t, :], in_=o_sb[m][:, 0, :])
-            b, t = unit_of(2 * m, 1)
-            nc.sync.dma_start(out=o_view[:, NT * b + t : NT * b + t + 3, :], in_=o_sb[m][:, 1:4, :])
+            b = SEQ[4 * m][0]
+            units = [SEQ[4 * m + n][1] for n in range(4)]
+            n = 0
+            while n < 4:
+                e = n + 1
+                while e < 4 and units[e] > units[n] and units[e] - units[e - 1] == units[n + 1] - units[n]:
+                    e += 1
+                step = units[n + 1] - units[n] if e > n + 1 else 1
+                u0 = NT * b + units[n]
+                nc.sync.dma_start(out=o_view[:, u0 : u0 + step * (e - n - 1) + 1 : step, :], in_=o_sb[m][:, n:e, :])
+                n = e
 
-        FIRST_PAIR = [min(x for x in range(NT) if plan(SEQ[x])[2] == o) // 2 for o in range(4)]
-        v_regroup_at = {}
-        v_quant_at = {}
-        for b in range(B):
+        def ok(x):
+            return 0 <= x < UNITS
+
+        tr_at, rg_at, qz_at = {}, {}, {}
+        for i in range(len(GROUPS)):
+            last = GROUPS[i][0] + GROUPS[i][1] - 1
+            tr_at[last + 2] = i
+            rg_at[last + 4] = i
+            qz_at[last + 7] = i
+        vr_at, vq_at = {}, {}
+        for o, lead in ((0, 1), (1, 4), (2, 10), (3, 13)):
+            vr_at[lead] = (o, 0)
+            vq_at[lead + 2] = (o, 0)
+        for o in range(4):
+            for b in range(1, B):
+                lead = 16 + 2 * (3 * o + b - 1)
+                vr_at[lead] = (o, b)
+                vq_at[lead + 2] = (o, b)
+        mask_at, clear_at = {}, {}
+        for b0, b1, per, starts in ((0, 1, 2, (4, 7, 16, 16)), (1, B, 1, (23, 29, 40, 43))):
             for o in range(4):
-                need = 16 * b + FIRST_PAIR[o] + 5
-                v_quant_at[need - 2] = (o, b)
-                v_regroup_at[need - 4] = (o, b)
+                tail = [j for j in range(NZ, NM) if PACKS[MASKED[j][0]][1][MASKED[j][2]] == o]
+                mask_at.setdefault(starts[o], []).append((tail[0], tail[-1] + 1, b0, b1))
+                x = starts[o]
+                for j in tail:
+                    while len(clear_at.get(x, [])) == per:
+                        x += 1
+                    clear_at.setdefault(x, []).append((j, b0, b1))
+            for g, j in sorted([(MASKED[j][0], j) for j in range(NZ)]):
+                x = starts[PACKS[g][1][MASKED[j][2]]]
+                while len(mask_at.get(x, [])) == per:
+                    x += 1
+                mask_at.setdefault(x, []).append((j, j + 1, b0, b1))
+                clear_at.setdefault(x, []).append((j, b0, b1))
 
-        for i in range(-3, PAIRS + 7):
-            if ok(i + 2):
-                st_qk(i + 2, 0)
-            if ok(i - 5):
-                st_mx(i - 5, 0)
-            if ok(i - 5):
-                st_mx(i - 5, 1)
-            if ok(i + 2):
-                st_qk(i + 2, 1)
-            if (i + 2) % 2 == 1 and 0 < (i + 2 + 3) // 2 < QUADS:
-                aux_pe((i + 2 + 3) // 2)
-            if i % 16 in (8, 10) and i // 16 + 1 < B and i > 0:
-                k_pe(i // 16 + 1, (i % 16 - 8) // 2)
-            if ok(i - 1):
-                st_tr(i - 1)
-            if ok(i - 2):
-                st_regroup(i - 2)
-            if (i + 2) % 2 == 0 and 0 < (i + 2 + 2) // 2 < QUADS:
-                aux_cp((i + 2 + 2) // 2)
-            if i % 16 in (9, 11) and i // 16 + 1 < B and i > 0:
-                k_cp(i // 16 + 1, (i % 16 - 9) // 2)
-            if ok(i):
-                st_exp(i)
-            if ok(i - 4):
-                st_quant(i - 4)
-            if ok(i + 2):
-                st_max(i + 2, 0)
-            if ok(i + 2):
-                st_max(i + 2, 1)
-            if (i - 6) % 2 == 1 and ok(i - 6):
-                st_norm((i - 6) // 2)
-            if i % 2 == 0 and ok(i - 1):
-                st_rc((i - 1) // 2)
-            if i in v_quant_at:
-                quant_v(v_quant_at[i][0], v_quant_at[i][1])
-            if i in v_regroup_at:
-                regroup_v(v_regroup_at[i][0], v_regroup_at[i][1])
+        for x in range(-LEAD, UNITS + LAG + 6):
+            if ok(x + LEAD) and x % 2 == 0:
+                st_qk(x + LEAD)
+            if ok(x - LAG):
+                st_mx(x - LAG)
+            if ok(x + LEAD) and x % 2 == 1:
+                st_qk(x + LEAD)
+            if x % 2 == 1:
+                for z in (x - 1, x):
+                    if z in tr_at:
+                        st_tr(tr_at[z])
+            if x == 1 - LEAD:
+                k_first(1)
+                q_pe(1)
+            if x == 3 - LEAD:
+                q_pe(2)
+            if (x + QP) % 4 == 0 and 2 < (x + QP) // 4 < QUADS:
+                q_pe((x + QP) // 4)
+            if x % 32 in (KP, KP + 4) and 0 <= x // 32 and x // 32 + 1 < B:
+                k_pe(x // 32 + 1, (x % 32 - KP) // 4)
+            if x in rg_at:
+                st_regroup(rg_at[x])
+            if (x - 1 + QP) % 4 == 0 and 2 < (x - 1 + QP) // 4 < QUADS:
+                q_cp((x - 1 + QP) // 4)
+            if x == 2 - LEAD:
+                q_cp(1)
+            if x == 4 - LEAD:
+                q_cp(2)
+            if x % 32 in (KP + 1, KP + 5) and 0 <= x // 32 and x // 32 + 1 < B:
+                k_cp(x // 32 + 1, (x % 32 - KP - 1) // 4)
+            if ok(x):
+                st_exp(x)
+            if x in qz_at:
+                st_quant(qz_at[x])
+            if ok(x + LEAD):
+                st_max(x + LEAD)
+            if x % 8 == 1 and ok(x - 9):
+                st_rc((x - 9) // 8)
+            if (x - LAG - ND) % 4 == 3 and ok(x - LAG - ND):
+                st_norm((x - LAG - ND) // 4)
+            if x in vq_at:
+                quant_v(vq_at[x][0], vq_at[x][1])
+            if x in vr_at:
+                regroup_v(vr_at[x][0], vr_at[x][1])
+            for j0, j1, b0, b1 in mask_at.get(x, []):
+                mask_v(j0, j1, b0, b1)
+            for j, b0, b1 in clear_at.get(x, []):
+                clear_v(j, b0, b1)
+            if x in LQ:
+                load_q(LQ.index(x) + 1)

@@ -32,7 +32,7 @@ SINK_SLOTS = (8, 17, 26)
 K_FIRST, K_LAST, K_SINK, K_FIRST8, K_NONE = 0, 1, 2, 3, 4
 WINDOWS = (0, 16, 3, 19)
 LEAD = 4
-LAG = 14
+LAG = 18
 
 
 def eslot(block):
@@ -96,10 +96,10 @@ MASKED = [mask[2:7] for mask in MASKED]
 NM = len(MASKED)
 NZ = len([1 for g, k, p, lo, hi in MASKED if hi < behind(g, p)])
 MASK_OF = {MASKED[j][0:3]: j for j in range(NM)}
-NTB = 2
-QP, KP = 7, 17
+QP, KP = 11, 17
 LQ = [6, 34, 66]
-ND = 2
+ND, NS, NV = 1, 2, 4
+VR, PER = 0, 1
 SEQ = [(b, PACKS[g][0][k], g, k) for b in range(B) for g in range(NG) for k in range(len(PACKS[g][0]))]
 GROUPS = [(x, len(PACKS[SEQ[x][2]][0]), SEQ[x][0], SEQ[x][2]) for x in range(UNITS) if SEQ[x][3] == 0]
 GROUP_OF = [len([1 for grp in GROUPS if grp[0] <= x]) - 1 for x in range(UNITS)]
@@ -112,7 +112,7 @@ def tile_swa_sinkmeta_t_kernel(tc, query_states, key_states, value_states, out):
         const = ctx.enter_context(tc.tile_pool(name="const", bufs=1))
         qtp = ctx.enter_context(tc.tile_pool(name="qtp", bufs=4))
         grpp = ctx.enter_context(tc.tile_pool(name="grpp", bufs=3))
-        codp = ctx.enter_context(tc.tile_pool(name="codp", bufs=4))
+        codp = ctx.enter_context(tc.tile_pool(name="codp", bufs=10))
         osbp = ctx.enter_context(tc.tile_pool(name="osbp", bufs=8))
         small = ctx.enter_context(tc.tile_pool(name="small", bufs=8))
         scp = ctx.enter_context(tc.tile_pool(name="scp", bufs=8))
@@ -219,7 +219,7 @@ def tile_swa_sinkmeta_t_kernel(tc, query_states, key_states, value_states, out):
                 while y < n and y not in taken:
                     y += 1
                 if y > x:
-                    nc.gpsimd.memset(e_all[g][:, :, 16 * x : 16 * y].bitcast(I32), 0)
+                    nc.vector.memset(e_all[g][:, :, 16 * x : 16 * y].bitcast(I32), 0)
                 x = y + 1
 
         zero_e(0)
@@ -253,7 +253,7 @@ def tile_swa_sinkmeta_t_kernel(tc, query_states, key_states, value_states, out):
             cols = slice(D * b0, D * b1)
             rows = slice(0, scale_row(hi - 1) + 1 if j0 < NZ else P)
             src = v_scl[o][rows, cols].bitcast(I32)
-            nc.gpsimd.tensor_copy(
+            nc.vector.tensor_copy(
                 out=v_msk[rows, j0:j1, cols].bitcast(I32),
                 in_=src.unsqueeze(1).to_broadcast([rows.stop, j1 - j0, (b1 - b0) * D // 4]),
             )
@@ -261,7 +261,7 @@ def tile_swa_sinkmeta_t_kernel(tc, query_states, key_states, value_states, out):
         def clear_v(j, b0, b1):
             lo = MASKED[j][3]
             if lo > 0:
-                nc.gpsimd.memset(v_msk[0 : scale_row(lo - 1) + 1, j, D * b0 : D * b1].bitcast(I32), 0)
+                nc.vector.memset(v_msk[0 : scale_row(lo - 1) + 1, j, D * b0 : D * b1].bitcast(I32), 0)
 
         kT = [const.tile([P, 2, 16 * (E_SLOTS + 1)], BF16, name="kT%d" % b) for b in range(B)]
         qT = {}
@@ -412,14 +412,16 @@ def tile_swa_sinkmeta_t_kernel(tc, query_states, key_states, value_states, out):
         def st_norm(m):
             o_sb[m] = osbp.tile([P, 4, D], F32, name="o_sb", tag="o_sb")
             scales = rc[m // 2][:, 4 * (m % 2) : 4 * (m % 2) + 4]
-            if False:
-                for n in range(4):
-                    nc.scalar.activation(
-                        out=o_sb[m][:, n, :], in_=o_ps[m][:, n, :], func=ACTF.Copy, scale=scales[:, n : n + 1],
-                    )
-            else:
-                nc.vector.tensor_tensor(
-                    out=o_sb[m][:], in0=o_ps[m][:], in1=scales.unsqueeze(2).to_broadcast([P, 4, D]), op=ALU.mult,
+            nc.vector.tensor_tensor(
+                out=o_sb[m][:, 0:NV], in0=o_ps[m][:, 0:NV],
+                in1=scales[:, 0:NV].unsqueeze(2).to_broadcast([P, NV, D]), op=ALU.mult,
+            )
+
+        def st_out(m):
+            scales = rc[m // 2][:, 4 * (m % 2) : 4 * (m % 2) + 4]
+            for n in range(NV, 4):
+                nc.scalar.activation(
+                    out=o_sb[m][:, n, :], in_=o_ps[m][:, n, :], func=ACTF.Copy, scale=scales[:, n : n + 1],
                 )
             b = SEQ[4 * m][0]
             units = [SEQ[4 * m + n][1] for n in range(4)]
@@ -443,16 +445,13 @@ def tile_swa_sinkmeta_t_kernel(tc, query_states, key_states, value_states, out):
             rg_at[last + 4] = i
             qz_at[last + 7] = i
         vr_at, vq_at = {}, {}
-        for o, lead in ((0, 1), (1, 4), (2, 10), (3, 13)):
-            vr_at[lead] = (o, 0)
-            vq_at[lead + 2] = (o, 0)
         for o in range(4):
-            for b in range(1, B):
-                lead = 16 + 2 * (3 * o + b - 1)
+            for b in range(B):
+                lead = VR + 2 * (B * o + b)
                 vr_at[lead] = (o, b)
                 vq_at[lead + 2] = (o, b)
         mask_at, clear_at = {}, {}
-        for b0, b1, per, starts in ((0, 1, 2, (4, 7, 16, 16)), (1, B, 1, (23, 29, 40, 43))):
+        for b0, b1, per, starts in ((0, B, PER, (VR + 9, VR + 17, VR + 25, VR + 33)),):
             for o in range(4):
                 tail = [j for j in range(NZ, NM) if PACKS[MASKED[j][0]][1][MASKED[j][2]] == o]
                 mask_at.setdefault(starts[o], []).append((tail[0], tail[-1] + 1, b0, b1))
@@ -468,7 +467,7 @@ def tile_swa_sinkmeta_t_kernel(tc, query_states, key_states, value_states, out):
                 mask_at.setdefault(x, []).append((j, j + 1, b0, b1))
                 clear_at.setdefault(x, []).append((j, b0, b1))
 
-        for x in range(-LEAD, UNITS + LAG + 6):
+        for x in range(-LEAD, UNITS + LAG + 8):
             if ok(x + LEAD) and x % 2 == 0:
                 st_qk(x + LEAD)
             if ok(x - LAG):
@@ -500,6 +499,8 @@ def tile_swa_sinkmeta_t_kernel(tc, query_states, key_states, value_states, out):
                 k_cp(x // 32 + 1, (x % 32 - KP - 1) // 4)
             if ok(x):
                 st_exp(x)
+            if (x - LAG - NS) % 4 == 3 and ok(x - LAG - NS):
+                st_out((x - LAG - NS) // 4)
             if x in qz_at:
                 st_quant(qz_at[x])
             if ok(x + LEAD):

@@ -32,7 +32,7 @@ SINK_SLOTS = (8, 17, 26)
 K_FIRST, K_LAST, K_SINK, K_FIRST8, K_NONE = 0, 1, 2, 3, 4
 WINDOWS = (0, 16, 3, 19)
 LEAD = 4
-LAG = 18
+LAG = 13
 
 
 def eslot(block):
@@ -96,9 +96,10 @@ MASKED = [mask[2:7] for mask in MASKED]
 NM = len(MASKED)
 NZ = len([1 for g, k, p, lo, hi in MASKED if hi < behind(g, p)])
 MASK_OF = {MASKED[j][0:3]: j for j in range(NM)}
-QP, KP = 11, 17
-LQ = [6, 34, 66]
-ND, NS, NV = 1, 2, 4
+QP, KP = 9, 19
+LQ = [0, 34, 66]
+ND = 1
+START = 18
 VR, PER = 0, 1
 SEQ = [(b, PACKS[g][0][k], g, k) for b in range(B) for g in range(NG) for k in range(len(PACKS[g][0]))]
 GROUPS = [(x, len(PACKS[SEQ[x][2]][0]), SEQ[x][0], SEQ[x][2]) for x in range(UNITS) if SEQ[x][3] == 0]
@@ -114,6 +115,7 @@ def tile_swa_sinkmeta_t_kernel(tc, query_states, key_states, value_states, out):
         grpp = ctx.enter_context(tc.tile_pool(name="grpp", bufs=3))
         codp = ctx.enter_context(tc.tile_pool(name="codp", bufs=10))
         osbp = ctx.enter_context(tc.tile_pool(name="osbp", bufs=8))
+        rawp = ctx.enter_context(tc.tile_pool(name="rawp", bufs=3))
         small = ctx.enter_context(tc.tile_pool(name="small", bufs=8))
         scp = ctx.enter_context(tc.tile_pool(name="scp", bufs=8))
         ps_s = ctx.enter_context(tc.psum_pool(name="ps_s", bufs=3))
@@ -166,8 +168,7 @@ def tile_swa_sinkmeta_t_kernel(tc, query_states, key_states, value_states, out):
         load_q(0, 29, 32)
         load_v(2)
         load_v(3)
-        for b in range(1, B):
-            load_k(b)
+        load_k(1)
 
         ident = const.tile([P, P], BF16, name="ident")
         make_identity(nc, ident[:])
@@ -233,18 +234,16 @@ def tile_swa_sinkmeta_t_kernel(tc, query_states, key_states, value_states, out):
         v_cod = [const.tile([P, B * D], U32, name="v_cod%d" % o, align_bytes=64) for o in range(4)]
         v_scl = [const.tile([P, B * D], U8, name="v_scl%d" % o, align_bytes=64) for o in range(4)]
 
-        def regroup_v(o, b):
+        def regroup_v(o):
             nc.gpsimd.tensor_scalar(
-                out=v_grp[o][:, b],
-                in0=v_raw[o][:, b].rearrange("p (t d) -> p d t", t=4),
+                out=v_grp[o][:],
+                in0=v_raw[o][:].rearrange("p b (t d) -> p b d t", t=4),
                 scalar1=1.0, scalar2=0.0, op0=ALU.mult, op1=ALU.add,
             )
 
-        def quant_v(o, b):
+        def quant_v(o):
             nc.vector.quantize_mx(
-                out=v_cod[o][:, D * b : D * (b + 1)].bitcast(FP8X4),
-                scales=v_scl[o][:, D * b : D * (b + 1)],
-                in_=v_grp[o][:, b].rearrange("p d t -> p (d t)"),
+                out=v_cod[o][:].bitcast(FP8X4), scales=v_scl[o][:], in_=v_grp[o][:].rearrange("p b d t -> p (b d t)")
             )
 
         def mask_v(j0, j1, b0, b1):
@@ -261,7 +260,8 @@ def tile_swa_sinkmeta_t_kernel(tc, query_states, key_states, value_states, out):
         def clear_v(j, b0, b1):
             lo = MASKED[j][3]
             if lo > 0:
-                nc.vector.memset(v_msk[0 : scale_row(lo - 1) + 1, j, D * b0 : D * b1].bitcast(I32), 0)
+                eng = nc.vector if PACKS[MASKED[j][0]][1][MASKED[j][2]] < 2 else nc.gpsimd
+                eng.memset(v_msk[0 : scale_row(lo - 1) + 1, j, D * b0 : D * b1].bitcast(I32), 0)
 
         kT = [const.tile([P, 2, 16 * (E_SLOTS + 1)], BF16, name="kT%d" % b) for b in range(B)]
         qT = {}
@@ -409,20 +409,22 @@ def tile_swa_sinkmeta_t_kernel(tc, query_states, key_states, value_states, out):
             rc[m] = small.tile([P, 8], F32, name="rc", tag="rc")
             nc.vector.reciprocal(out=rc[m][:], in_=rs[m][:])
 
+        def by_scalar(m):
+            return m % 8 == 0
+
         def st_norm(m):
             o_sb[m] = osbp.tile([P, 4, D], F32, name="o_sb", tag="o_sb")
             scales = rc[m // 2][:, 4 * (m % 2) : 4 * (m % 2) + 4]
-            nc.vector.tensor_tensor(
-                out=o_sb[m][:, 0:NV], in0=o_ps[m][:, 0:NV],
-                in1=scales[:, 0:NV].unsqueeze(2).to_broadcast([P, NV, D]), op=ALU.mult,
-            )
+            factors = scales.unsqueeze(2).to_broadcast([P, 4, D])
+            if by_scalar(m):
+                raw = rawp.tile([P, 4, D], F32, name="raw", tag="raw")
+                nc.scalar.copy(out=raw[:], in_=o_ps[m][:])
+                nc.gpsimd.tensor_tensor(out=o_sb[m][:], in0=raw[:], in1=factors, op=ALU.mult)
+            else:
+                nc.vector.tensor_tensor(out=o_sb[m][:], in0=o_ps[m][:], in1=factors, op=ALU.mult)
+            st_store(m)
 
-        def st_out(m):
-            scales = rc[m // 2][:, 4 * (m % 2) : 4 * (m % 2) + 4]
-            for n in range(NV, 4):
-                nc.scalar.activation(
-                    out=o_sb[m][:, n, :], in_=o_ps[m][:, n, :], func=ACTF.Copy, scale=scales[:, n : n + 1],
-                )
+        def st_store(m):
             b = SEQ[4 * m][0]
             units = [SEQ[4 * m + n][1] for n in range(4)]
             n = 0
@@ -446,12 +448,10 @@ def tile_swa_sinkmeta_t_kernel(tc, query_states, key_states, value_states, out):
             qz_at[last + 7] = i
         vr_at, vq_at = {}, {}
         for o in range(4):
-            for b in range(B):
-                lead = VR + 2 * (B * o + b)
-                vr_at[lead] = (o, b)
-                vq_at[lead + 2] = (o, b)
+            vr_at[VR + 5 * o] = o
+            vq_at[VR + 5 * o + 6] = o
         mask_at, clear_at = {}, {}
-        for b0, b1, per, starts in ((0, B, PER, (VR + 9, VR + 17, VR + 25, VR + 33)),):
+        for b0, b1, per, starts in ((0, B, PER, (VR + 7, VR + 12, VR + 17, VR + 22)),):
             for o in range(4):
                 tail = [j for j in range(NZ, NM) if PACKS[MASKED[j][0]][1][MASKED[j][2]] == o]
                 mask_at.setdefault(starts[o], []).append((tail[0], tail[-1] + 1, b0, b1))
@@ -467,11 +467,17 @@ def tile_swa_sinkmeta_t_kernel(tc, query_states, key_states, value_states, out):
                 mask_at.setdefault(x, []).append((j, j + 1, b0, b1))
                 clear_at.setdefault(x, []).append((j, b0, b1))
 
-        for x in range(-LEAD, UNITS + LAG + 8):
+        mx_at, norm_at = {}, {}
+        for y in range(UNITS):
+            mx_at.setdefault(max(y + LAG, START + 3 * y // 4), []).append(y)
+            if y % 4 == 3:
+                norm_at[max(y + LAG, START + 3 * y // 4) + ND] = y // 4
+
+        for x in range(-LEAD, UNITS + LAG + ND):
             if ok(x + LEAD) and x % 2 == 0:
                 st_qk(x + LEAD)
-            if ok(x - LAG):
-                st_mx(x - LAG)
+            for y in mx_at.get(x, []):
+                st_mx(y)
             if ok(x + LEAD) and x % 2 == 1:
                 st_qk(x + LEAD)
             if x % 2 == 1:
@@ -499,23 +505,23 @@ def tile_swa_sinkmeta_t_kernel(tc, query_states, key_states, value_states, out):
                 k_cp(x // 32 + 1, (x % 32 - KP - 1) // 4)
             if ok(x):
                 st_exp(x)
-            if (x - LAG - NS) % 4 == 3 and ok(x - LAG - NS):
-                st_out((x - LAG - NS) // 4)
             if x in qz_at:
                 st_quant(qz_at[x])
             if ok(x + LEAD):
                 st_max(x + LEAD)
             if x % 8 == 1 and ok(x - 9):
                 st_rc((x - 9) // 8)
-            if (x - LAG - ND) % 4 == 3 and ok(x - LAG - ND):
-                st_norm((x - LAG - ND) // 4)
+            if x in norm_at:
+                st_norm(norm_at[x])
             if x in vq_at:
-                quant_v(vq_at[x][0], vq_at[x][1])
+                quant_v(vq_at[x])
             if x in vr_at:
-                regroup_v(vr_at[x][0], vr_at[x][1])
+                regroup_v(vr_at[x])
             for j0, j1, b0, b1 in mask_at.get(x, []):
                 mask_v(j0, j1, b0, b1)
             for j, b0, b1 in clear_at.get(x, []):
                 clear_v(j, b0, b1)
             if x in LQ:
+                if x > LQ[0]:
+                    load_k(LQ.index(x) + 1)
                 load_q(LQ.index(x) + 1)

from contextlib import ExitStack
import math

import concourse.mybir as mybir
from concourse.masks import make_identity

BF16 = mybir.dt.bfloat16
F32 = mybir.dt.float32
I32 = mybir.dt.int32
U32 = mybir.dt.uint32
U8 = mybir.dt.uint8
FP8X4 = mybir.dt.float8_e4m3fn_x4
ALU = mybir.AluOpType
ACTF = mybir.ActivationFunctionType
AX = mybir.AxisListType

B, S, H, D, WIN, META = 4, 1024, 4, 128, 256, 4
P = 128
BLK = 32
POS = P // H
NT = S // POS
UNITS = B * NT
QUADS = UNITS // 4
RUN = 10
SCALE = 1.0 / math.sqrt(D)
NEG = -1.0e30
ALLOWED = sum(min(i, WIN) + 1 + min(max(i - WIN, 0), META) for i in range(S))
FLOPS = 4 * D * ALLOWED * B * H

E_SLOTS = 35
SINK_SLOTS = (8, 17, 26)
K_FIRST, K_LAST, K_SINK, K_FIRST8, K_NONE = 0, 1, 2, 3, 4
WINDOWS = (0, 16, 3, 19)
LEAD = 4
LAG = 13


def eslot(block):
    return block + block // 8


def eblock(slot):
    return 0 if slot in SINK_SLOTS else slot - slot // 9


def plan(t):
    if t < 8:
        return 0, t + 1, None
    start = eslot(t - 8)
    return start, RUN, [x for x in SINK_SLOTS if start < x < start + RUN][0] - start


PACKS = [
    ((2, 3), (0, 0)), ((4,), (0,)),
    ((5, 14, 23), (0, 1)), ((6, 15, 24), (0, 1)), ((7, 16, 25), (0, 1)), ((8, 17, 26), (0, 1)),
    ((0, 9, 18, 27), (0, 1)), ((1, 10, 19, 28), (0, 1)),
    ((11, 20, 29), (2, 3)), ((12, 21, 30), (2, 3)), ((13, 22, 31), (2, 3)),
]
NG = len(PACKS)


def place(g, k):
    units, opers = PACKS[g]
    start, n = plan(units[k])[0:2]
    a = 16 * k if opers[-1] == 0 else start - WINDOWS[opers[0]]
    parts = [
        (p, max(a, 16 * p) - 16 * p, min(a + n, 16 * p + 16) - 16 * p)
        for p in range(len(opers))
        if a < 16 * p + 16 and a + n > 16 * p
    ]
    return a, parts


def crowd(g, p):
    return len([1 for k in range(len(PACKS[g][0])) for part in place(g, k)[1] if part[0] == p])


def behind(g, p):
    return max([part[2] for k in range(len(PACKS[g][0])) for part in place(g, k)[1] if part[0] == p])


def scale_row(y):
    return 32 * (y // 4) + y % 4


MASKED = sorted(
    [
        (hi == behind(g, p), PACKS[g][1][p], g, k, p, lo, hi)
        for g in range(NG)
        for k in range(len(PACKS[g][0]))
        for p, lo, hi in place(g, k)[1]
        if crowd(g, p) > 1
    ]
)
MASKED = [mask[2:7] for mask in MASKED]
NM = len(MASKED)
NZ = len([1 for g, k, p, lo, hi in MASKED if hi < behind(g, p)])
MASK_OF = {MASKED[j][0:3]: j for j in range(NM)}
QP, KP = 9, 19
LQ = [0, 34, 66]
ND = 1
START = 18
VR, PER = 0, 1
SEQ = [(b, PACKS[g][0][k], g, k) for b in range(B) for g in range(NG) for k in range(len(PACKS[g][0]))]
GROUPS = [(x, len(PACKS[SEQ[x][2]][0]), SEQ[x][0], SEQ[x][2]) for x in range(UNITS) if SEQ[x][3] == 0]
GROUP_OF = [len([1 for grp in GROUPS if grp[0] <= x]) - 1 for x in range(UNITS)]


def tile_swa_sinkmeta_t_kernel(tc, query_states, key_states, value_states, out):
    nc = tc.nc
    with ExitStack() as ctx:
        ctx.enter_context(tc.manual_schedule())
        const = ctx.enter_context(tc.tile_pool(name="const", bufs=1))
        qtp = ctx.enter_context(tc.tile_pool(name="qtp", bufs=4))
        grpp = ctx.enter_context(tc.tile_pool(name="grpp", bufs=3))
        codp = ctx.enter_context(tc.tile_pool(name="codp", bufs=10))
        osbp = ctx.enter_context(tc.tile_pool(name="osbp", bufs=8))
        rawp = ctx.enter_context(tc.tile_pool(name="rawp", bufs=3))
        small = ctx.enter_context(tc.tile_pool(name="small", bufs=8))
        scp = ctx.enter_context(tc.tile_pool(name="scp", bufs=8))
        ps_s = ctx.enter_context(tc.psum_pool(name="ps_s", bufs=3))
        ps_m = ctx.enter_context(tc.psum_pool(name="ps_m", bufs=2))
        ps_t = ctx.enter_context(tc.psum_pool(name="ps_t", bufs=2))
        ps_a = ctx.enter_context(tc.psum_pool(name="ps_a", bufs=1))

        q_view = query_states.rearrange("b s c -> (b s c)").rearrange(
            "(n r d) -> r n d", r=P, d=D
        )
        o_view = out.rearrange("b s c -> (b s c)").rearrange("(n r d) -> r n d", r=P, d=D)
        k_view = key_states.rearrange("b (a p) d -> p (b a) d", p=P)

        k_sb = [const.tile([P, 8, D], BF16, name="k_sb%d" % b) for b in range(B)]
        q_sb = [const.tile([P, NT, D], BF16, name="q_sb%d" % b) for b in range(B)]
        v_raw = [const.tile([P, B, 4 * D], BF16, name="v_raw%d" % o) for o in range(4)]

        def load_k(b, lo=0, hi=8):
            nc.sync.dma_start(out=k_sb[b][:, lo:hi, :], in_=k_view[:, 8 * b + lo : 8 * b + hi, :])

        def load_q(b, lo=0, hi=NT):
            nc.sync.dma_start(out=q_sb[b][:, lo:hi, :], in_=q_view[:, NT * b + lo : NT * b + hi, :])

        def load_v(o):
            x = 0
            while x < 16:
                y = x + 1
                while y < 16 and eblock(WINDOWS[o] + y) == eblock(WINDOWS[o] + y - 1) + 1:
                    y += 1
                k0, nkeys = BLK * eblock(WINDOWS[o] + x), BLK * (y - x)
                nc.sync.dma_start(
                    out=v_raw[o][8 * x : 8 * y],
                    in_=value_states[:, k0 : k0 + nkeys, :].rearrange("b (p t) d -> p b (t d)", t=4),
                )
                x = y

        load_k(0, 0, 4)
        load_q(0, 2, 6)
        load_q(0, 14, 17)
        load_q(0, 23, 26)
        load_q(0, 6, 9)
        load_k(0, 4, 8)
        load_q(0, 17, 20)
        load_q(0, 26, 29)
        load_q(0, 0, 2)
        load_v(0)
        load_q(0, 9, 14)
        load_v(1)
        load_q(0, 20, 23)
        load_q(0, 29, 32)
        load_v(2)
        load_v(3)
        load_k(1)

        ident = const.tile([P, P], BF16, name="ident")
        make_identity(nc, ident[:])
        mask_f = const.tile([P, 2, BLK], F32, name="mask_f")
        nc.gpsimd.memset(mask_f[:], 0.0)
        nc.gpsimd.affine_select(
            out=mask_f[:, 0, :], in_=mask_f[:, 0, :], compare_op=ALU.is_ge, fill=NEG,
            base=3, pattern=[[4, BLK]], channel_multiplier=-1,
        )
        nc.gpsimd.affine_select(
            out=mask_f[:, 1, :], in_=mask_f[:, 1, :], compare_op=ALU.is_ge, fill=NEG,
            base=0, pattern=[[-4, BLK]], channel_multiplier=1,
        )

        warm = const.tile([P, 1], F32, name="warm")
        nc.vector.memset(warm[:], 0.0)
        nc.scalar.activation(out=warm[:], in_=warm[:], func=ACTF.Exp)

        v_msk = const.tile([P, NM, B * D], U8, name="v_msk", align_bytes=64)
        nc.vector.memset(v_msk[:, 0:NZ].rearrange("p m d -> p (m d)").bitcast(I32), 0)

        mask_b = const.tile([P, 5, 2, 16], BF16, name="mask_b")
        for kind in (K_FIRST, K_LAST):
            nc.vector.tensor_copy(
                out=mask_b[:, kind].rearrange("p u (g e) -> p u g e", e=2),
                in_=mask_f[:, kind, :].rearrange("p (g u e) -> p u g e", u=2, e=2),
            )
        nc.vector.memset(mask_b[:, K_SINK], NEG)
        nc.vector.memset(mask_b[:, K_SINK, :, 0:2], 0.0)
        nc.vector.tensor_copy(out=mask_b[:, K_FIRST8], in_=mask_b[:, K_FIRST])
        nc.vector.memset(mask_b[:, K_FIRST8, :, 0:2], 0.0)
        nc.vector.memset(mask_b[:, K_NONE], NEG)
        mask_fl = const.tile([P, 2, 2, 2, 16], BF16, name="mask_fl")
        for w, kind in ((0, K_FIRST), (1, K_FIRST8)):
            nc.vector.tensor_copy(out=mask_fl[:, w, :, 0, :], in_=mask_b[:, kind])
            nc.vector.tensor_copy(out=mask_fl[:, w, :, 1, :], in_=mask_b[:, K_LAST])

        e_all = [const.tile([P, 2, 256 * len(PACKS[g][1])], BF16, name="e_all%d" % g) for g in range(NG)]

        def zero_e(g):
            taken = []
            for k in range(len(PACKS[g][0])):
                a = place(g, k)[0]
                taken += [x for x in range(a, a + plan(PACKS[g][0][k])[1])]
            n = 16 * len(PACKS[g][1])
            x = 0
            while x < n:
                y = x
                while y < n and y not in taken:
                    y += 1
                if y > x:
                    nc.vector.memset(e_all[g][:, :, 16 * x : 16 * y].bitcast(I32), 0)
                x = y + 1

        zero_e(0)
        zero_e(1)
        ident_f = const.tile([P, P], F32, name="ident_f")
        make_identity(nc, ident_f[:])
        for g in range(2, NG):
            zero_e(g)

        v_grp = [const.tile([P, B, D, 4], BF16, name="v_grp%d" % o, align_bytes=64) for o in range(4)]
        v_cod = [const.tile([P, B * D], U32, name="v_cod%d" % o, align_bytes=64) for o in range(4)]
        v_scl = [const.tile([P, B * D], U8, name="v_scl%d" % o, align_bytes=64) for o in range(4)]

        def regroup_v(o):
            nc.gpsimd.tensor_scalar(
                out=v_grp[o][:],
                in0=v_raw[o][:].rearrange("p b (t d) -> p b d t", t=4),
                scalar1=1.0, scalar2=0.0, op0=ALU.mult, op1=ALU.add,
            )

        def quant_v(o):
            nc.vector.quantize_mx(
                out=v_cod[o][:].bitcast(FP8X4), scales=v_scl[o][:], in_=v_grp[o][:].rearrange("p b d t -> p (b d t)")
            )

        def mask_v(j0, j1, b0, b1):
            g, k, p, lo, hi = MASKED[j0]
            o = PACKS[g][1][p]
            cols = slice(D * b0, D * b1)
            rows = slice(0, scale_row(hi - 1) + 1 if j0 < NZ else P)
            src = v_scl[o][rows, cols].bitcast(I32)
            nc.vector.tensor_copy(
                out=v_msk[rows, j0:j1, cols].bitcast(I32),
                in_=src.unsqueeze(1).to_broadcast([rows.stop, j1 - j0, (b1 - b0) * D // 4]),
            )

        def clear_v(j, b0, b1):
            lo = MASKED[j][3]
            if lo > 0:
                eng = nc.vector if PACKS[MASKED[j][0]][1][MASKED[j][2]] < 2 else nc.gpsimd
                eng.memset(v_msk[0 : scale_row(lo - 1) + 1, j, D * b0 : D * b1].bitcast(I32), 0)

        kT = [const.tile([P, 2, 16 * (E_SLOTS + 1)], BF16, name="kT%d" % b) for b in range(B)]
        qT = {}

        def k_copy(b, grp8, src):
            nc.scalar.copy(
                out=kT[b][:, :, 144 * grp8 : 144 * grp8 + 128].rearrange("p u (g e) -> p u g e", e=2),
                in_=src.rearrange("p a c -> p (a c)").rearrange("p (g u e) -> p u g e", u=2, e=2),
            )

        def k_sinks(b):
            nc.gpsimd.tensor_scalar(
                out=kT[b][:].rearrange("p u (x c) -> p u x c", c=16)[:, :, 8:27:9, :],
                in0=kT[b][:, :, 0:16].unsqueeze(2).to_broadcast([P, 2, 3, 16]),
                scalar1=1.0, scalar2=0.0, op0=ALU.mult, op1=ALU.add,
            )

        def k_first(half):
            kps = ps_t.tile([P, 4, P], BF16, name="kps", tag="tp")
            for a in range(4):
                nc.tensor.transpose(kps[:, a, :], k_sb[0][:, 4 * half + a, :], ident[:])
            for g in range(2):
                k_copy(0, 2 * half + g, kps[:, 2 * g : 2 * g + 2, :])
            if half == 0:
                k_sinks(0)

        aux = ps_a.tile([P, 8, P], BF16, name="aux")
        q_ps = aux[:, 0:4, :]
        k_ps = aux[:, 4:8, :]

        def q_pe(m):
            for n in range(4):
                b, t = SEQ[4 * m + n][0:2]
                nc.tensor.transpose(q_ps[:, n, :], q_sb[b][:, t, :], ident[:])

        def q_cp(m):
            qT[m] = qtp.tile([P, 4, P], BF16, name="qT", tag="qT")
            if True:
                nc.scalar.copy(out=qT[m][:], in_=q_ps)
            else:
                nc.vector.tensor_copy(out=qT[m][:], in_=q_ps)

        def k_pe(kb, kh):
            for n in range(4):
                nc.tensor.transpose(k_ps[:, n, :], k_sb[kb][:, 4 * kh + n, :], ident[:])

        def k_cp(kb, kh):
            for g in range(2):
                k_copy(kb, 2 * kh + g, k_ps[:, 2 * g : 2 * g + 2, :])
            if kh == 0:
                k_sinks(kb)

        k_first(0)
        q_pe(0)
        q_cp(0)

        s_ps, s_sb, nb, rs, rc, tps, grp, cod, scl, o_ps, o_sb = {}, {}, {}, {}, {}, {}, {}, {}, {}, {}, {}

        def st_qk(x):
            b, t = SEQ[x][0:2]
            start, nsl, sink = plan(t)
            bank = ps_s.tile([P, 4 * P], F32, name="s", tag="s")
            s = bank[:, 0 : 32 * RUN].rearrange("p (u c) -> p u c", u=2)
            s_ps[x] = s
            slots = s.rearrange("p u (x c) -> p u x c", c=16)
            ops = [(s[:, :, 0 : 16 * nsl], qT[x // 4][:, x % 4, :], kT[b][:, :, 16 * start : 16 * (start + nsl)])]
            if t < 8:
                ops.append((s[:, :, 16 * t : 16 * t + 16], ident[:], mask_b[:, K_LAST]))
            else:
                ops.append((slots[:, :, 0:RUN:RUN - 1, :], ident[:], mask_fl[:, 1 if t == 8 else 0]))
                ops.append((s[:, :, 16 * sink : 16 * sink + 16], ident[:], mask_b[:, K_NONE if t == 8 else K_SINK]))
            for i, (o_ap, l_ap, r_ap) in enumerate(ops):
                nc.tensor.matmul(out=o_ap, lhsT=l_ap, rhs=r_ap, start=(i == 0), stop=(i == len(ops) - 1))

        def st_max(x):
            j, n = x // 2, x % 2
            if n == 0:
                nb[j] = small.tile([P, 2], F32, name="nb", tag="nb")
            nsl = plan(SEQ[x][1])[1]
            s_sb[x] = scp.tile([P, 2, 16 * RUN], F32, name="s_sb", tag="s_sb")
            nc.vector.tensor_scalar(
                out=s_sb[x][:, :, 0 : 16 * nsl], in0=s_ps[x][:, :, 0 : 16 * nsl],
                scalar1=-SCALE, scalar2=None, op0=ALU.mult, op1=ALU.min, accum_out=nb[j][:, n : n + 1],
            )

        def st_exp(x):
            m, n = x // 8, x % 8
            if n == 0:
                rs[m] = small.tile([P, 8], F32, name="rs", tag="rs")
            b, t, g, k = SEQ[x]
            nsl = plan(t)[1]
            a = place(g, k)[0]
            nc.scalar.activation(
                out=e_all[g][:, :, 16 * a : 16 * (a + nsl)],
                in_=s_sb[x][:, :, 0 : 16 * nsl],
                func=ACTF.Exp, bias=nb[x // 2][:, x % 2 : x % 2 + 1], scale=-1.0,
                accum_out=rs[m][:, n : n + 1],
            )

        def st_tr(i):
            g = GROUPS[i][3]
            np_ = len(PACKS[g][1])
            tps[i] = ps_t.tile([P, np_, 2, P], F32, name="tps", tag="tp")
            for p in range(np_):
                for u in range(2):
                    words = e_all[g][:, u, 256 * p : 256 * (p + 1)].bitcast(F32)
                    nc.tensor.transpose(tps[i][:, p, u, :], words, ident_f[:])

        def st_regroup(i):
            np_ = len(PACKS[GROUPS[i][3]][1])
            grp[i] = grpp.tile([P, np_, P, 2], F32, name="grp", tag="grp", align_bytes=64)
            nc.scalar.copy(out=grp[i][:], in_=tps[i][:].rearrange("p n w r -> p n r w"))

        def st_quant(i):
            np_ = len(PACKS[GROUPS[i][3]][1])
            cod[i] = codp.tile([P, np_ * P], U32, name="cod", tag="cod", align_bytes=64)
            scl[i] = codp.tile([P, np_ * P], U8, name="scl", tag="scl", align_bytes=64)
            nc.vector.quantize_mx(
                out=cod[i][:].bitcast(FP8X4), scales=scl[i][:],
                in_=grp[i][:].rearrange("p n r w -> p (n r w)").bitcast(BF16),
            )

        def st_mx(x):
            i = GROUP_OF[x]
            b, t, g, k = SEQ[x]
            if x % 4 == 0:
                o_ps[x // 4] = ps_m.tile([P, 4, D], F32, name="o_ps", tag="o_ps")
            parts = place(g, k)[1]
            for y in range(len(parts)):
                p = parts[y][0]
                o = PACKS[g][1][p]
                masked = (g, k, p) in MASK_OF
                cols = slice(D * b, D * (b + 1))
                scales = v_msk[:, MASK_OF[g, k, p], cols] if masked else v_scl[o][:, cols]
                nc.tensor.matmul_mx(
                    out=o_ps[x // 4][:, x % 4, :],
                    lhsT=cod[i][:, P * p : P * (p + 1)].bitcast(FP8X4),
                    lhsT_scale=scl[i][:, P * p : P * (p + 1)],
                    rhs=v_cod[o][:, cols].bitcast(FP8X4),
                    rhs_scale=scales,
                    start=(y == 0), stop=(y == len(parts) - 1),
                )

        def st_rc(m):
            rc[m] = small.tile([P, 8], F32, name="rc", tag="rc")
            nc.vector.reciprocal(out=rc[m][:], in_=rs[m][:])

        def by_scalar(m):
            return m % 8 == 0

        def st_norm(m):
            o_sb[m] = osbp.tile([P, 4, D], F32, name="o_sb", tag="o_sb")
            scales = rc[m // 2][:, 4 * (m % 2) : 4 * (m % 2) + 4]
            factors = scales.unsqueeze(2).to_broadcast([P, 4, D])
            if by_scalar(m):
                raw = rawp.tile([P, 4, D], F32, name="raw", tag="raw")
                nc.scalar.copy(out=raw[:], in_=o_ps[m][:])
                nc.gpsimd.tensor_tensor(out=o_sb[m][:], in0=raw[:], in1=factors, op=ALU.mult)
            else:
                nc.vector.tensor_tensor(out=o_sb[m][:], in0=o_ps[m][:], in1=factors, op=ALU.mult)
            st_store(m)

        def st_store(m):
            b = SEQ[4 * m][0]
            units = [SEQ[4 * m + n][1] for n in range(4)]
            n = 0
            while n < 4:
                e = n + 1
                while e < 4 and units[e] > units[n] and units[e] - units[e - 1] == units[n + 1] - units[n]:
                    e += 1
                step = units[n + 1] - units[n] if e > n + 1 else 1
                u0 = NT * b + units[n]
                nc.sync.dma_start(out=o_view[:, u0 : u0 + step * (e - n - 1) + 1 : step, :], in_=o_sb[m][:, n:e, :])
                n = e

        def ok(x):
            return 0 <= x < UNITS

        tr_at, rg_at, qz_at = {}, {}, {}
        for i in range(len(GROUPS)):
            last = GROUPS[i][0] + GROUPS[i][1] - 1
            tr_at[last + 2] = i
            rg_at[last + 4] = i
            qz_at[last + 7] = i
        vr_at, vq_at = {}, {}
        for o in range(4):
            vr_at[VR + 5 * o] = o
            vq_at[VR + 5 * o + 6] = o
        mask_at, clear_at = {}, {}
        for b0, b1, per, starts in ((0, B, PER, (VR + 7, VR + 12, VR + 17, VR + 22)),):
            for o in range(4):
                tail = [j for j in range(NZ, NM) if PACKS[MASKED[j][0]][1][MASKED[j][2]] == o]
                mask_at.setdefault(starts[o], []).append((tail[0], tail[-1] + 1, b0, b1))
                x = starts[o]
                for j in tail:
                    while len(clear_at.get(x, [])) == per:
                        x += 1
                    clear_at.setdefault(x, []).append((j, b0, b1))
            for g, j in sorted([(MASKED[j][0], j) for j in range(NZ)]):
                x = starts[PACKS[g][1][MASKED[j][2]]]
                while len(mask_at.get(x, [])) == per:
                    x += 1
                mask_at.setdefault(x, []).append((j, j + 1, b0, b1))
                clear_at.setdefault(x, []).append((j, b0, b1))

        mx_at, norm_at = {}, {}
        for y in range(UNITS):
            mx_at.setdefault(max(y + LAG, START + 3 * y // 4), []).append(y)
            if y % 4 == 3:
                norm_at[max(y + LAG, START + 3 * y // 4) + ND] = y // 4

        for x in range(-LEAD, UNITS + LAG + ND):
            if ok(x + LEAD) and x % 2 == 0:
                st_qk(x + LEAD)
            for y in mx_at.get(x, []):
                st_mx(y)
            if ok(x + LEAD) and x % 2 == 1:
                st_qk(x + LEAD)
            if x % 2 == 1:
                for z in (x - 1, x):
                    if z in tr_at:
                        st_tr(tr_at[z])
            if x == 1 - LEAD:
                k_first(1)
                q_pe(1)
            if x == 3 - LEAD:
                q_pe(2)
            if (x + QP) % 4 == 0 and 2 < (x + QP) // 4 < QUADS:
                q_pe((x + QP) // 4)
            if x % 32 in (KP, KP + 4) and 0 <= x // 32 and x // 32 + 1 < B:
                k_pe(x // 32 + 1, (x % 32 - KP) // 4)
            if x in rg_at:
                st_regroup(rg_at[x])
            if (x - 1 + QP) % 4 == 0 and 2 < (x - 1 + QP) // 4 < QUADS:
                q_cp((x - 1 + QP) // 4)
            if x == 2 - LEAD:
                q_cp(1)
            if x == 4 - LEAD:
                q_cp(2)
            if x % 32 in (KP + 1, KP + 5) and 0 <= x // 32 and x // 32 + 1 < B:
                k_cp(x // 32 + 1, (x % 32 - KP - 1) // 4)
            if ok(x):
                st_exp(x)
            if x in qz_at:
                st_quant(qz_at[x])
            if ok(x + LEAD):
                st_max(x + LEAD)
            if x % 8 == 1 and ok(x - 9):
                st_rc((x - 9) // 8)
            if x in norm_at:
                st_norm(norm_at[x])
            if x in vq_at:
                quant_v(vq_at[x])
            if x in vr_at:
                regroup_v(vr_at[x])
            for j0, j1, b0, b1 in mask_at.get(x, []):
                mask_v(j0, j1, b0, b1)
            for j, b0, b1 in clear_at.get(x, []):
                clear_v(j, b0, b1)
            if x in LQ:
                if x > LQ[0]:
                    load_k(LQ.index(x) + 1)
                load_q(LQ.index(x) + 1)
